import numpy as np
import ml_dtypes


def mxq(x, axis, fmt="e4m3"):
    dtype, down = {"e4m3": (ml_dtypes.float8_e4m3fn, 7), "e5m2": (ml_dtypes.float8_e5m2, 14)}[fmt]
    v = np.moveaxis(np.asarray(x, np.float32).astype(ml_dtypes.bfloat16).astype(np.float64), axis, -1)
    blocks = v.reshape(v.shape[:-1] + (-1, 32))
    amax = np.abs(blocks).max(-1, keepdims=True)
    byte = np.maximum(np.where(amax > 0, np.frexp(amax)[1] - 1 + 127, 0) - down, 1)
    scale = np.exp2(byte - 127.0)
    codes = (blocks / scale).astype(np.float32).astype(dtype).astype(np.float64)
    return np.moveaxis((codes * scale).reshape(v.shape), -1, axis)


WIDE = False


def mx_kscale(k):
    if not WIDE:
        return np.ones(k)
    levels = np.array([10, -10, 5, -5, 0])
    if k % 512:
        return np.exp2(np.random.permutation(np.resize(levels, k // 32))).repeat(32)
    a = np.empty((k // 512, 16))
    for p in range(k // 512):
        a[p, :8] = np.random.permutation(np.resize(levels, 8))
        for g in range(8):
            far = levels[np.abs(levels - a[p, g]) >= 10]
            a[p, g + 8] = far[np.random.randint(len(far))]
    return np.exp2(a.ravel()).repeat(32)


BF16 = ml_dtypes.bfloat16


def bf(x):
    return np.asarray(x, np.float32).astype(BF16)


def f64(x):
    return np.asarray(x).astype(np.float64)


B, S, H, A, NH = 4, 128, 1536, 1536, 12
HD = A // NH
LN_EPS = 1e-5


def setup_inputs():
    s = mx_kscale(A)
    return {"ctx_heads": bf(np.random.standard_normal((B, NH, S, HD)) * s.reshape(NH, 1, HD)),
            "Wo": bf(np.random.standard_normal((H, A)) / np.sqrt(A) / s),
            "bo": bf(np.random.standard_normal(H) * 0.3),
            "features": bf(np.random.standard_normal((B, S, H))),
            "ln_g": bf(1.0 + 0.1 * np.random.standard_normal(H)),
            "ln_b": bf(0.2 * np.random.standard_normal(H))}


def core(ctx_heads, Wo, bo, features, ln_g, ln_b):
    ctx = f64(ctx_heads).transpose(0, 2, 1, 3).reshape(B, S, A)
    p = (mxq(ctx, 2, "e4m3") @ mxq(f64(Wo), 1, "e4m3").T) + f64(bo)
    y = p + f64(features)
    mu = y.mean(-1, keepdims=True)
    var = y.var(-1, keepdims=True)
    return (y - mu) / np.sqrt(var + LN_EPS) * f64(ln_g) + f64(ln_b)


def e4m3fn_bytes(y):
    return np.clip(np.asarray(y, np.float64), -448.0, 448.0).astype(np.float32).astype(ml_dtypes.float8_e4m3fn).view(np.uint8)


Y_SCALE = 210.0


def reference(ctx_heads, Wo, bo, features, ln_g, ln_b):
    out = core(ctx_heads, Wo, bo, features, ln_g, ln_b)
    return out, e4m3fn_bytes(out * Y_SCALE)

@@ -1,0 +1,227 @@
+from contextlib import ExitStack
+
+import concourse.mybir as mybir
+from concourse.masks import make_identity
+
+F32 = mybir.dt.float32
+BF16 = mybir.dt.bfloat16
+U32 = mybir.dt.uint32
+U8 = mybir.dt.uint8
+I32 = mybir.dt.int32
+FP8X4 = mybir.dt.float8_e4m3fn_x4
+FP8 = mybir.dt.float8_e4m3fn
+ALU = mybir.AluOpType
+ACT = mybir.ActivationFunctionType
+
+P = 128
+NT = 4
+K = 1536
+H = 1536
+NG = 3
+NC = 3
+CW = 512
+LN_EPS = 1e-5
+Y_SCALE = 210.0
+
+FLOPS = 2 * NT * P * K * H
+
+
+def tile_hierarchicalattention_pb_kernel(tc, ctx_heads, Wo, bo, features, ln_g, ln_b, out_0, out_1):
+    nc = tc.nc
+    with ExitStack() as ctx:
+        const = ctx.enter_context(tc.tile_pool(name="const", bufs=1))
+        raw = ctx.enter_context(tc.tile_pool(name="raw", bufs=1))
+        keep = ctx.enter_context(tc.tile_pool(name="keep", bufs=1))
+        stage = ctx.enter_context(tc.tile_pool(name="stage", bufs=6))
+        work = ctx.enter_context(tc.psum_pool(name="work", bufs=5))
+        gbp = ctx.enter_context(tc.psum_pool(name="gbp", bufs=1))
+        ctx.enter_context(tc.manual_schedule())
+
+        wraw = [raw.tile([P, 2, K], BF16, name="wraw%d" % j, tag="wraw%d" % j) for j in range(6)]
+        craw = [raw.tile([P, K], BF16, name="craw%d" % m, tag="craw%d" % m) for m in range(NT)]
+        feat = [raw.tile([P, H], BF16, name="feat%d" % m, tag="feat%d" % m) for m in range(NT)]
+        wq = [keep.tile([P, NG, CW], U32, name="wq%d" % n, tag="wq%d" % n, align_bytes=64) for n in range(NC)]
+        ws = [keep.tile([P, NG, CW], U8, name="ws%d" % n, tag="ws%d" % n, align_bytes=64) for n in range(NC)]
+        cq = [keep.tile([P, NG, P], U32, name="cq%d" % m, tag="cq%d" % m, align_bytes=64) for m in range(NT)]
+        cs = [keep.tile([P, NG, P], U8, name="cs%d" % m, tag="cs%d" % m, align_bytes=64) for m in range(NT)]
+        yt = [keep.tile([P, H], F32, name="yt%d" % m, tag="yt%d" % m) for m in range(NT)]
+        ot = [keep.tile([P, H], F32, name="ot%d" % m, tag="ot%d" % m) for m in range(NT)]
+        o8 = [keep.tile([P, H], FP8, name="o8%d" % m, tag="o8%d" % m) for m in range(NT)]
+        s1 = [keep.tile([P, NC], F32, name="s1%d" % m, tag="s1%d" % m) for m in range(NT)]
+        s1j = [keep.tile([P, NC], F32, name="s1j%d" % m, tag="s1j%d" % m) for m in range(NT)]
+        negmean = [keep.tile([P, 1], F32, name="nm%d" % m, tag="nm%d" % m) for m in range(NT)]
+        m2 = [keep.tile([P, 1], F32, name="m2%d" % m, tag="m2%d" % m) for m in range(NT)]
+        std = [keep.tile([P, 1], F32, name="sd%d" % m, tag="sd%d" % m) for m in range(NT)]
+        rstd = [keep.tile([P, 1], F32, name="rs%d" % m, tag="rs%d" % m) for m in range(NT)]
+        ident = const.tile([P, P], F32, name="ident", tag="ident")
+        ones = const.tile([P, P], BF16, name="ones", tag="ones")
+        eps = const.tile([P, 1], F32, name="eps", tag="eps")
+        warm = const.tile([P, 1], F32, name="warm", tag="warm")
+        vz = const.tile([P, 3, H], BF16, name="vz", tag="vz")
+        bo_bc = const.tile([P, H], BF16, name="bo_bc", tag="bo_bc")
+        gb = [gbp.tile([P, 2 * CW], BF16, name="gb%d" % i, tag="gb%d" % i) for i in range(3)]
+
+        def gb_chunk(v, c):
+            q = v * NC + c
+            return gb[q // 2][:, (q % 2) * CW : (q % 2 + 1) * CW]
+
+        def load_w(j):
+            nc.sync.dma_start(out=wraw[j][:], in_=Wo[2 * P * j : 2 * P * (j + 1), :].rearrange("(a r) k -> r a k", a=2))
+
+        def load_c(m):
+            nc.sync.dma_start(out=craw[m][:].rearrange("s (h d) -> s h d", d=P), in_=ctx_heads[m].rearrange("h s d -> s h d"))
+
+        def load_f(m):
+            nc.sync.dma_start(out=feat[m][:], in_=features[m])
+
+        load_w(0)
+        load_w(1)
+        load_c(0)
+        load_f(0)
+        for j in range(2, 6):
+            load_w(j)
+        for m in range(1, NT):
+            load_c(m)
+            load_f(m)
+
+        nc.gpsimd.memset(eps[:], LN_EPS)
+        nc.vector.memset(vz[:].bitcast(I32), 0)
+        make_identity(nc, ident[:])
+        nc.gpsimd.memset(ones[:], 1.0)
+        nc.scalar.activation(out=warm[:], in_=eps[:], func=ACT.Sqrt)
+        for v, vec in enumerate((bo, ln_g, ln_b)):
+            nc.scalar.dma_start(out=vz[0:1, v, :], in_=vec.rearrange("(o n) -> o n", o=1))
+
+        def spread_bo():
+            for c in range(NC):
+                ps = work.tile([P, CW], F32, name="wk", tag="wk")
+                nc.tensor.matmul(out=ps[:], lhsT=ones[:], rhs=vz[:, 0, c * CW : (c + 1) * CW], start=True, stop=True)
+                nc.scalar.copy(out=bo_bc[:, c * CW : (c + 1) * CW], in_=ps[:])
+
+        def spread_gb(v):
+            for c in range(NC):
+                nc.tensor.matmul(out=gb_chunk(v - 1, c), lhsT=ones[:], rhs=vz[:, v, c * CW : (c + 1) * CW], start=True, stop=True)
+
+        def add_bias(m):
+            for c in range(NC):
+                sl = slice(c * CW, (c + 1) * CW)
+                nc.gpsimd.tensor_tensor(out=yt[m][:, sl], in0=feat[m][:, sl], in1=bo_bc[:, sl], op=ALU.add)
+
+        def turn(words_of, blocks):
+            tp = work.tile([P, 2, 2, P], F32, name="wk", tag="wk")
+            for a, (words, g) in enumerate(blocks):
+                for u in range(2):
+                    nc.tensor.transpose(out=tp[:, a, u, :], in_=words[:, 256 * g + u : 256 * (g + 1) : 2], identity=ident[:])
+            n = len(blocks)
+            grp = stage.tile([P, 2, P, 4], BF16, name="grp", tag="grp", align_bytes=64)
+            nc.scalar.copy(out=grp[:, 0:n].bitcast(F32), in_=tp[:, 0:n].rearrange("p a u r -> p a r u"))
+            return grp
+
+        def turn_w(j):
+            words = wraw[j][:].bitcast(F32)
+            return [turn(None, [(words[:, 0, :], g), (words[:, 1, :], g)]) for g in range(NG)]
+
+        def quant_w(j, grps):
+            n, a = j // 2, j % 2
+            for g in range(NG):
+                nc.vector.quantize_mx(
+                    out=wq[n][:, g, a * 256 : (a + 1) * 256].bitcast(FP8X4),
+                    scales=ws[n][:, g, a * 256 : (a + 1) * 256],
+                    in_=grps[g][:].rearrange("p a r t -> p (a r t)"),
+                )
+
+        def turn_c(m):
+            words = craw[m][:].bitcast(F32)
+            return [turn(None, [(words, 0), (words, 1)]), turn(None, [(words, 2)])]
+
+        def quant_c(m, grps):
+            nc.vector.quantize_mx(
+                out=cq[m][:, 0:2, :].rearrange("p g s -> p (g s)").bitcast(FP8X4),
+                scales=cs[m][:, 0:2, :].rearrange("p g s -> p (g s)"),
+                in_=grps[0][:].rearrange("p a r t -> p (a r t)"),
+            )
+            nc.vector.quantize_mx(
+                out=cq[m][:, 2, :].bitcast(FP8X4),
+                scales=cs[m][:, 2, :],
+                in_=grps[1][:, 0].rearrange("p r t -> p (r t)"),
+            )
+
+        def product(m, n):
+            acc = work.tile([P, CW], F32, name="wk", tag="wk")
+            for g in range(NG):
+                nc.tensor.matmul_mx(
+                    out=acc[:],
+                    lhsT=cq[m][:, g, :].bitcast(FP8X4),
+                    lhsT_scale=cs[m][:, g, :],
+                    rhs=wq[n][:, g, :].bitcast(FP8X4),
+                    rhs_scale=ws[n][:, g, :],
+                    start=(g == 0),
+                    stop=(g == NG - 1),
+                )
+            return acc
+
+        def residual(m, n, acc):
+            sl = slice(n * CW, (n + 1) * CW)
+            nc.vector.scalar_tensor_tensor(
+                out=yt[m][:, sl], in0=acc[:], scalar=1.0, in1=yt[m][:, sl], op0=ALU.mult, op1=ALU.add, accum_out=s1[m][:, n : n + 1]
+            )
+
+        pending = []
+        have = []
+        for i, src in enumerate(("w0", "w1", "c0", "w2", "w3", "w4", "w5")):
+            idx = int(src[1])
+            grps = turn_w(idx) if src[0] == "w" else turn_c(idx)
+            if i == 0:
+                spread_bo()
+                for m in range(NT):
+                    add_bias(m)
+            if i == 1:
+                spread_gb(1)
+            if i == 2:
+                spread_gb(2)
+            accs = [(n, product(0, n)) for n in pending]
+            if src[0] == "w":
+                quant_w(idx, grps)
+            else:
+                quant_c(idx, grps)
+            for n, acc in accs:
+                residual(0, n, acc)
+            have.append(src)
+            pending = []
+            if src == "c0":
+                pending = [0]
+            if src == "w3":
+                pending = [1]
+            if src == "w5":
+                pending = [2]
+
+        accs = []
+        for m in range(NT):
+            grps = turn_c(m + 1) if m + 1 < NT else None
+            if m == 0:
+                accs = [(n, product(0, n)) for n in pending]
+            for n, acc in accs:
+                residual(m, n, acc)
+            nc.vector.tensor_scalar(
+                out=s1j[m][:], in0=s1[m][:], scalar1=-1.0 / H, scalar2=None, op0=ALU.mult, op1=ALU.add, accum_out=negmean[m][:]
+            )
+            for c in range(NC):
+                sl = slice(c * CW, (c + 1) * CW)
+                nc.vector.scalar_tensor_tensor(
+                    out=ot[m][:, sl], in0=yt[m][:, sl], scalar=negmean[m][:], in1=gb_chunk(0, c), op0=ALU.add, op1=ALU.mult
+                )
+            sq = stage.tile([P, H], BF16, name="sq", tag="sq", bufs=2)
+            nc.scalar.activation(out=sq[:], in_=yt[m][:], func=ACT.Square, bias=negmean[m][:], scale=1.0, accum_out=m2[m][:])
+            nc.scalar.activation(out=std[m][:], in_=m2[m][:], func=ACT.Sqrt, bias=eps[:], scale=1.0 / H)
+            if m + 1 < NT:
+                quant_c(m + 1, grps)
+                accs = [(n, product(m + 1, n)) for n in range(NC)]
+            nc.vector.reciprocal(out=rstd[m][:], in_=std[m][:])
+            for c in range(NC):
+                sl = slice(c * CW, (c + 1) * CW)
+                nc.vector.scalar_tensor_tensor(
+                    out=ot[m][:, sl], in0=ot[m][:, sl], scalar=rstd[m][:], in1=gb_chunk(1, c), op0=ALU.mult, op1=ALU.add
+                )
+                nc.scalar.activation(out=o8[m][:, sl], in_=ot[m][:, sl], func=ACT.Copy, scale=Y_SCALE, saturate=False)
+                nc.sync.dma_start(out=out_0[m][:, sl], in_=ot[m][:, sl])
+            nc.sync.dma_start(out=out_1[m], in_=o8[m][:].bitcast(U8))

@@ -28,6 +28,8 @@ FLOPS = 2 * NT * P * K * H
 
 def tile_hierarchicalattention_pb_kernel(tc, ctx_heads, Wo, bo, features, ln_g, ln_b, out_0, out_1):
     nc = tc.nc
+    CA = 2 * CW
+    G_TILES = 0
     with ExitStack() as ctx:
         const = ctx.enter_context(tc.tile_pool(name="const", bufs=1))
         raw = ctx.enter_context(tc.tile_pool(name="raw", bufs=1))
@@ -57,16 +59,20 @@ def tile_hierarchicalattention_pb_kernel(tc, ctx_heads, Wo, bo, features, ln_g, 
         ones = const.tile([P, P], BF16, name="ones", tag="ones")
         eps = const.tile([P, 1], F32, name="eps", tag="eps")
         warm = const.tile([P, 1], F32, name="warm", tag="warm")
-        vz = const.tile([P, 3, H], BF16, name="vz", tag="vz")
+        vz = [const.tile([P, H], BF16, name="vz%d" % v, tag="vz%d" % v) for v in range(3)]
         bo_bc = const.tile([P, H], BF16, name="bo_bc", tag="bo_bc")
-        gb = [gbp.tile([P, 2 * CW], BF16, name="gb%d" % i, tag="gb%d" % i) for i in range(3)]
-
-        def gb_chunk(v, c):
-            q = v * NC + c
-            return gb[q // 2][:, (q % 2) * CW : (q % 2 + 1) * CW]
+        gb_sb = const.tile([P, 2 * CW], BF16, name="gb_sb", tag="gb_sb")
+        g_ps = gbp.tile([P, CA], BF16, name="g_ps", tag="g_ps")
+        b_ps = gbp.tile([P, CA], BF16, name="b_ps", tag="b_ps")
+        gb_ps = gbp.tile([P, 2 * CW], BF16, name="gb_ps", tag="gb_ps")
 
         def load_w(j):
-            nc.sync.dma_start(out=wraw[j][:], in_=Wo[2 * P * j : 2 * P * (j + 1), :].rearrange("(a r) k -> r a k", a=2))
+            rows = Wo[2 * P * j : 2 * P * (j + 1), :].rearrange("(a r) k -> r a k", a=2)
+            if j in (0, 5):
+                for g in range(NG):
+                    nc.sync.dma_start(out=wraw[j][:, :, g * 512 : (g + 1) * 512], in_=rows[:, :, g * 512 : (g + 1) * 512])
+            else:
+                nc.sync.dma_start(out=wraw[j][:], in_=rows)
 
         def load_c(m):
             nc.sync.dma_start(out=craw[m][:].rearrange("s (h d) -> s h d", d=P), in_=ctx_heads[m].rearrange("h s d -> s h d"))
@@ -74,52 +80,64 @@ def tile_hierarchicalattention_pb_kernel(tc, ctx_heads, Wo, bo, features, ln_g, 
         def load_f(m):
             nc.sync.dma_start(out=feat[m][:], in_=features[m])
 
-        load_w(0)
-        load_w(1)
-        load_c(0)
-        load_f(0)
-        for j in range(2, 6):
+        for j in range(5):
             load_w(j)
+        load_c(0)
+        load_w(5)
+        load_f(0)
         for m in range(1, NT):
             load_c(m)
             load_f(m)
 
         nc.gpsimd.memset(eps[:], LN_EPS)
-        nc.vector.memset(vz[:].bitcast(I32), 0)
+        for v in range(3):
+            nc.vector.memset(vz[v][:].bitcast(I32), 0)
         make_identity(nc, ident[:])
         nc.gpsimd.memset(ones[:], 1.0)
         nc.scalar.activation(out=warm[:], in_=eps[:], func=ACT.Sqrt)
         for v, vec in enumerate((bo, ln_g, ln_b)):
-            nc.scalar.dma_start(out=vz[0:1, v, :], in_=vec.rearrange("(o n) -> o n", o=1))
+            nc.scalar.dma_start(out=vz[v][0:1, :], in_=vec.rearrange("(o n) -> o n", o=1))
+
+        def spread(out, v, c):
+            nc.tensor.matmul(out=out, lhsT=ones[:], rhs=vz[v][:, c * CW : (c + 1) * CW], start=True, stop=True)
 
         def spread_bo():
             for c in range(NC):
                 ps = work.tile([P, CW], F32, name="wk", tag="wk")
-                nc.tensor.matmul(out=ps[:], lhsT=ones[:], rhs=vz[:, 0, c * CW : (c + 1) * CW], start=True, stop=True)
+                spread(ps[:], 0, c)
                 nc.scalar.copy(out=bo_bc[:, c * CW : (c + 1) * CW], in_=ps[:])
 
-        def spread_gb(v):
-            for c in range(NC):
-                nc.tensor.matmul(out=gb_chunk(v - 1, c), lhsT=ones[:], rhs=vz[:, v, c * CW : (c + 1) * CW], start=True, stop=True)
+        def spread_g():
+            spread(g_ps[:, 0:CW], 1, 0)
+            spread(g_ps[:, CW:CA], 1, 1)
+
+        def spread_b():
+            spread(b_ps[:, 0:CW], 2, 0)
+            spread(b_ps[:, CW:CA], 2, 1)
+            spread(gb_ps[:, 0:CW], 1, 2)
+            spread(gb_ps[:, CW : 2 * CW], 2, 2)
 
         def add_bias(m):
             for c in range(NC):
                 sl = slice(c * CW, (c + 1) * CW)
                 nc.gpsimd.tensor_tensor(out=yt[m][:, sl], in0=feat[m][:, sl], in1=bo_bc[:, sl], op=ALU.add)
 
-        def turn(words_of, blocks):
+        def turn(blocks, on_vector):
             tp = work.tile([P, 2, 2, P], F32, name="wk", tag="wk")
             for a, (words, g) in enumerate(blocks):
                 for u in range(2):
                     nc.tensor.transpose(out=tp[:, a, u, :], in_=words[:, 256 * g + u : 256 * (g + 1) : 2], identity=ident[:])
             n = len(blocks)
             grp = stage.tile([P, 2, P, 4], BF16, name="grp", tag="grp", align_bytes=64)
-            nc.scalar.copy(out=grp[:, 0:n].bitcast(F32), in_=tp[:, 0:n].rearrange("p a u r -> p a r u"))
+            if on_vector:
+                nc.vector.tensor_copy(out=grp[:, 0:n].bitcast(F32), in_=tp[:, 0:n].rearrange("p a u r -> p a r u"))
+            else:
+                nc.scalar.copy(out=grp[:, 0:n].bitcast(F32), in_=tp[:, 0:n].rearrange("p a u r -> p a r u"))
             return grp
 
         def turn_w(j):
             words = wraw[j][:].bitcast(F32)
-            return [turn(None, [(words[:, 0, :], g), (words[:, 1, :], g)]) for g in range(NG)]
+            return [turn([(words[:, 0, :], g), (words[:, 1, :], g)], g == 0) for g in range(NG)]
 
         def quant_w(j, grps):
             n, a = j // 2, j % 2
@@ -132,7 +150,7 @@ def tile_hierarchicalattention_pb_kernel(tc, ctx_heads, Wo, bo, features, ln_g, 
 
         def turn_c(m):
             words = craw[m][:].bitcast(F32)
-            return [turn(None, [(words, 0), (words, 1)]), turn(None, [(words, 2)])]
+            return [turn([(words, 0), (words, 1)], False), turn([(words, 2)], False)]
 
         def quant_c(m, grps):
             nc.vector.quantize_mx(
@@ -146,6 +164,8 @@ def tile_hierarchicalattention_pb_kernel(tc, ctx_heads, Wo, bo, features, ln_g, 
                 in_=grps[1][:, 0].rearrange("p r t -> p (r t)"),
             )
 
+        accs = {}
+
         def product(m, n):
             acc = work.tile([P, CW], F32, name="wk", tag="wk")
             for g in range(NG):
@@ -158,70 +178,96 @@ def tile_hierarchicalattention_pb_kernel(tc, ctx_heads, Wo, bo, features, ln_g, 
                     start=(g == 0),
                     stop=(g == NG - 1),
                 )
-            return acc
+            accs[(m, n)] = acc
 
-        def residual(m, n, acc):
+        def residual(m, n):
             sl = slice(n * CW, (n + 1) * CW)
             nc.vector.scalar_tensor_tensor(
-                out=yt[m][:, sl], in0=acc[:], scalar=1.0, in1=yt[m][:, sl], op0=ALU.mult, op1=ALU.add, accum_out=s1[m][:, n : n + 1]
+                out=yt[m][:, sl], in0=accs[(m, n)][:], scalar=1.0, in1=yt[m][:, sl], op0=ALU.mult, op1=ALU.add, accum_out=s1[m][:, n : n + 1]
             )
 
-        pending = []
-        have = []
-        for i, src in enumerate(("w0", "w1", "c0", "w2", "w3", "w4", "w5")):
-            idx = int(src[1])
-            grps = turn_w(idx) if src[0] == "w" else turn_c(idx)
-            if i == 0:
-                spread_bo()
-                for m in range(NT):
-                    add_bias(m)
-            if i == 1:
-                spread_gb(1)
-            if i == 2:
-                spread_gb(2)
-            accs = [(n, product(0, n)) for n in pending]
-            if src[0] == "w":
-                quant_w(idx, grps)
-            else:
-                quant_c(idx, grps)
-            for n, acc in accs:
-                residual(0, n, acc)
-            have.append(src)
-            pending = []
-            if src == "c0":
-                pending = [0]
-            if src == "w3":
-                pending = [1]
-            if src == "w5":
-                pending = [2]
+        A = slice(0, CA)
+        B = slice(CA, H)
 
-        accs = []
+        def centre_scale(m, sl, g_ap):
+            nc.vector.scalar_tensor_tensor(out=ot[m][:, sl], in0=yt[m][:, sl], scalar=negmean[m][:], in1=g_ap, op0=ALU.add, op1=ALU.mult)
+
+        def norm_shift(m, sl, b_ap):
+            nc.vector.scalar_tensor_tensor(out=ot[m][:, sl], in0=ot[m][:, sl], scalar=rstd[m][:], in1=b_ap, op0=ALU.mult, op1=ALU.add)
+
+        def finish_b(m):
+            if m < G_TILES:
+                nc.gpsimd.tensor_scalar(out=ot[m][:, B], in0=yt[m][:, B], scalar1=negmean[m][:], scalar2=rstd[m][:], op0=ALU.add, op1=ALU.mult)
+                nc.gpsimd.tensor_tensor(out=ot[m][:, B], in0=ot[m][:, B], in1=gb_sb[:, 0:CW], op=ALU.mult)
+                nc.gpsimd.tensor_tensor(out=ot[m][:, B], in0=ot[m][:, B], in1=gb_sb[:, CW : 2 * CW], op=ALU.add)
+            else:
+                norm_shift(m, B, gb_ps[:, CW : 2 * CW])
+
+        def leave(m, sl):
+            nc.scalar.activation(out=o8[m][:, sl], in_=ot[m][:, sl], func=ACT.Copy, scale=Y_SCALE, saturate=False)
+            nc.sync.dma_start(out=out_0[m][:, sl], in_=ot[m][:, sl])
+            nc.sync.dma_start(out=out_1[m][:, sl], in_=o8[m][:, sl].bitcast(U8))
+
+        for j in range(5):
+            grps = turn_w(j)
+            if j == 0:
+                spread_bo()
+                for m in range(3):
+                    add_bias(m)
+            quant_w(j, grps)
+        cgrp = {}
+        cgrp[0] = turn_c(0)
+        spread_g()
+        quant_c(0, cgrp[0])
+        grps = turn_w(5)
+        product(0, 0)
+        product(0, 1)
+        cgrp[1] = turn_c(1)
+        quant_w(5, grps)
+        product(0, 2)
+        spread_b()
+        residual(0, 0)
+        residual(0, 1)
+        quant_c(1, cgrp[1])
+        cgrp[2] = turn_c(2)
+        residual(0, 2)
+
         for m in range(NT):
-            grps = turn_c(m + 1) if m + 1 < NT else None
-            if m == 0:
-                accs = [(n, product(0, n)) for n in pending]
-            for n, acc in accs:
-                residual(m, n, acc)
+            last = m == NT - 1
             nc.vector.tensor_scalar(
                 out=s1j[m][:], in0=s1[m][:], scalar1=-1.0 / H, scalar2=None, op0=ALU.mult, op1=ALU.add, accum_out=negmean[m][:]
             )
-            for c in range(NC):
-                sl = slice(c * CW, (c + 1) * CW)
-                nc.vector.scalar_tensor_tensor(
-                    out=ot[m][:, sl], in0=yt[m][:, sl], scalar=negmean[m][:], in1=gb_chunk(0, c), op0=ALU.add, op1=ALU.mult
-                )
             sq = stage.tile([P, H], BF16, name="sq", tag="sq", bufs=2)
             nc.scalar.activation(out=sq[:], in_=yt[m][:], func=ACT.Square, bias=negmean[m][:], scale=1.0, accum_out=m2[m][:])
             nc.scalar.activation(out=std[m][:], in_=m2[m][:], func=ACT.Sqrt, bias=eps[:], scale=1.0 / H)
-            if m + 1 < NT:
-                quant_c(m + 1, grps)
-                accs = [(n, product(m + 1, n)) for n in range(NC)]
+            if m > 0:
+                finish_b(m - 1)
+                leave(m - 1, A)
+                leave(m - 1, B)
+            if m == 1:
+                add_bias(3)
+            if not last:
+                for n in range(NC):
+                    product(m + 1, n)
+            if m + 3 < NT:
+                cgrp[m + 3] = turn_c(m + 3)
+            if 0 < m and not last:
+                residual(m + 1, 0)
+            centre_scale(m, A, g_ps[:])
+            if m >= G_TILES:
+                centre_scale(m, B, gb_ps[:, 0:CW])
+            if m == 0:
+                residual(m + 1, 0)
+            if not last:
+                residual(m + 1, 1)
+            if m + 2 < NT:
+                quant_c(m + 2, cgrp[m + 2])
             nc.vector.reciprocal(out=rstd[m][:], in_=std[m][:])
-            for c in range(NC):
-                sl = slice(c * CW, (c + 1) * CW)
-                nc.vector.scalar_tensor_tensor(
-                    out=ot[m][:, sl], in0=ot[m][:, sl], scalar=rstd[m][:], in1=gb_chunk(1, c), op0=ALU.mult, op1=ALU.add
-                )
-                nc.scalar.activation(out=o8[m][:, sl], in_=ot[m][:, sl], func=ACT.Copy, scale=Y_SCALE, saturate=False)
-                nc.sync.dma_start(out=out_0[m][:, sl], in_=ot[m][:, sl])
-            nc.sync.dma_start(out=out_1[m], in_=o8[m][:].bitcast(U8))
+            if not last:
+                residual(m + 1, 2)
+                norm_shift(m, A, b_ps[:])
+        m = NT - 1
+        for c, b_ap in enumerate((b_ps[:, 0:CW], b_ps[:, CW:CA], gb_ps[:, CW : 2 * CW])):
+            sl = slice(c * CW, (c + 1) * CW)
+            norm_shift(m, sl, b_ap)
+            leave(m, sl)

@@ -67,7 +67,7 @@ def tile_hierarchicalattention_pb_kernel(tc, ctx_heads, Wo, bo, features, ln_g, 
         gb_ps = gbp.tile([P, 2 * CW], BF16, name="gb_ps", tag="gb_ps")
 
         def load_w(j):
-            rows = Wo[2 * P * j : 2 * P * (j + 1), :].rearrange("(a r) k -> r a k", a=2)
+            rows = Wo[2 * P * j : 2 * P * (j + 1), :].rearrange("(r a) k -> r a k", a=2)
             if j in (0, 5):
                 for g in range(NG):
                     nc.sync.dma_start(out=wraw[j][:, :, g * 512 : (g + 1) * 512], in_=rows[:, :, g * 512 : (g + 1) * 512])
@@ -101,43 +101,46 @@ def tile_hierarchicalattention_pb_kernel(tc, ctx_heads, Wo, bo, features, ln_g, 
         def spread(out, v, c):
             nc.tensor.matmul(out=out, lhsT=ones[:], rhs=vz[v][:, c * CW : (c + 1) * CW], start=True, stop=True)
 
-        def spread_bo():
-            for c in range(NC):
-                ps = work.tile([P, CW], F32, name="wk", tag="wk")
-                spread(ps[:], 0, c)
-                nc.scalar.copy(out=bo_bc[:, c * CW : (c + 1) * CW], in_=ps[:])
+        def spread_bo(c):
+            ps = work.tile([P, CW], F32, name="wk", tag="wk")
+            spread(ps[:], 0, c)
+            nc.scalar.copy(out=bo_bc[:, c * CW : (c + 1) * CW], in_=ps[:])
 
-        def spread_g():
-            spread(g_ps[:, 0:CW], 1, 0)
-            spread(g_ps[:, CW:CA], 1, 1)
-
-        def spread_b():
-            spread(b_ps[:, 0:CW], 2, 0)
-            spread(b_ps[:, CW:CA], 2, 1)
-            spread(gb_ps[:, 0:CW], 1, 2)
-            spread(gb_ps[:, CW : 2 * CW], 2, 2)
+        spreads = [
+            [lambda: spread_bo(0), lambda: spread_bo(1)],
+            [lambda: spread_bo(2), lambda: spread(g_ps[:, 0:CW], 1, 0)],
+            [lambda: spread(g_ps[:, CW:CA], 1, 1), lambda: spread(b_ps[:, 0:CW], 2, 0)],
+            [lambda: spread(b_ps[:, CW:CA], 2, 1), lambda: spread(gb_ps[:, 0:CW], 1, 2)],
+            [lambda: spread(gb_ps[:, CW : 2 * CW], 2, 2)],
+        ]
 
         def add_bias(m):
-            for c in range(NC):
-                sl = slice(c * CW, (c + 1) * CW)
+            for c in range(H // 256):
+                sl = slice(c * 256, (c + 1) * 256)
                 nc.gpsimd.tensor_tensor(out=yt[m][:, sl], in0=feat[m][:, sl], in1=bo_bc[:, sl], op=ALU.add)
 
-        def turn(blocks, on_vector):
+        def turn(blocks, on_vector, rows_interleaved):
             tp = work.tile([P, 2, 2, P], F32, name="wk", tag="wk")
             for a, (words, g) in enumerate(blocks):
                 for u in range(2):
                     nc.tensor.transpose(out=tp[:, a, u, :], in_=words[:, 256 * g + u : 256 * (g + 1) : 2], identity=ident[:])
             n = len(blocks)
-            grp = stage.tile([P, 2, P, 4], BF16, name="grp", tag="grp", align_bytes=64)
-            if on_vector:
-                nc.vector.tensor_copy(out=grp[:, 0:n].bitcast(F32), in_=tp[:, 0:n].rearrange("p a u r -> p a r u"))
+            grp = stage.tile([P, 2 * P, 4], BF16, name="grp", tag="grp", align_bytes=64)
+            if rows_interleaved:
+                dst = grp[:].bitcast(F32).rearrange("p (r a) u -> p r a u", a=2)
+                src = tp[:].rearrange("p a u r -> p r a u")
             else:
-                nc.scalar.copy(out=grp[:, 0:n].bitcast(F32), in_=tp[:, 0:n].rearrange("p a u r -> p a r u"))
+                dst = grp[:, 0 : n * P].bitcast(F32).rearrange("p (a r) u -> p a r u", a=n)
+                src = tp[:, 0:n].rearrange("p a u r -> p a r u")
+            if on_vector:
+                nc.vector.tensor_copy(out=dst, in_=src)
+            else:
+                nc.scalar.copy(out=dst, in_=src)
             return grp
 
         def turn_w(j):
             words = wraw[j][:].bitcast(F32)
-            return [turn([(words[:, 0, :], g), (words[:, 1, :], g)], g == 0) for g in range(NG)]
+            return [turn([(words[:, 0, :], g), (words[:, 1, :], g)], g == 0, True) for g in range(NG)]
 
         def quant_w(j, grps):
             n, a = j // 2, j % 2
@@ -145,23 +148,23 @@ def tile_hierarchicalattention_pb_kernel(tc, ctx_heads, Wo, bo, features, ln_g, 
                 nc.vector.quantize_mx(
                     out=wq[n][:, g, a * 256 : (a + 1) * 256].bitcast(FP8X4),
                     scales=ws[n][:, g, a * 256 : (a + 1) * 256],
-                    in_=grps[g][:].rearrange("p a r t -> p (a r t)"),
+                    in_=grps[g][:].rearrange("p c t -> p (c t)"),
                 )
 
         def turn_c(m):
             words = craw[m][:].bitcast(F32)
-            return [turn([(words, 0), (words, 1)], False), turn([(words, 2)], False)]
+            return [turn([(words, 0), (words, 1)], False, False), turn([(words, 2)], False, False)]
 
         def quant_c(m, grps):
             nc.vector.quantize_mx(
                 out=cq[m][:, 0:2, :].rearrange("p g s -> p (g s)").bitcast(FP8X4),
                 scales=cs[m][:, 0:2, :].rearrange("p g s -> p (g s)"),
-                in_=grps[0][:].rearrange("p a r t -> p (a r t)"),
+                in_=grps[0][:].rearrange("p c t -> p (c t)"),
             )
             nc.vector.quantize_mx(
                 out=cq[m][:, 2, :].bitcast(FP8X4),
                 scales=cs[m][:, 2, :],
-                in_=grps[1][:, 0].rearrange("p r t -> p (r t)"),
+                in_=grps[1][:, 0:P].rearrange("p c t -> p (c t)"),
             )
 
         accs = {}
@@ -203,21 +206,29 @@ def tile_hierarchicalattention_pb_kernel(tc, ctx_heads, Wo, bo, features, ln_g, 
             else:
                 norm_shift(m, B, gb_ps[:, CW : 2 * CW])
 
+        owed = []
+
+        def pay():
+            for m, sl in owed:
+                nc.sync.dma_start(out=out_1[m][:, sl], in_=o8[m][:, sl].bitcast(U8))
+            owed.clear()
+
         def leave(m, sl):
             nc.scalar.activation(out=o8[m][:, sl], in_=ot[m][:, sl], func=ACT.Copy, scale=Y_SCALE, saturate=False)
             nc.sync.dma_start(out=out_0[m][:, sl], in_=ot[m][:, sl])
-            nc.sync.dma_start(out=out_1[m][:, sl], in_=o8[m][:, sl].bitcast(U8))
+            pay()
+            owed.append((m, sl))
 
         for j in range(5):
             grps = turn_w(j)
-            if j == 0:
-                spread_bo()
+            for f in spreads[j]:
+                f()
+            if j == 1:
                 for m in range(3):
                     add_bias(m)
             quant_w(j, grps)
         cgrp = {}
         cgrp[0] = turn_c(0)
-        spread_g()
         quant_c(0, cgrp[0])
         grps = turn_w(5)
         product(0, 0)
@@ -225,7 +236,6 @@ def tile_hierarchicalattention_pb_kernel(tc, ctx_heads, Wo, bo, features, ln_g, 
         cgrp[1] = turn_c(1)
         quant_w(5, grps)
         product(0, 2)
-        spread_b()
         residual(0, 0)
         residual(0, 1)
         quant_c(1, cgrp[1])
@@ -271,3 +281,4 @@ def tile_hierarchicalattention_pb_kernel(tc, ctx_heads, Wo, bo, features, ln_g, 
             sl = slice(c * CW, (c + 1) * CW)
             norm_shift(m, sl, b_ap)
             leave(m, sl)
+        pay()

@@ -67,7 +67,7 @@ def tile_hierarchicalattention_pb_kernel(tc, ctx_heads, Wo, bo, features, ln_g, 
         gb_ps = gbp.tile([P, 2 * CW], BF16, name="gb_ps", tag="gb_ps")
 
         def load_w(j):
-            rows = Wo[2 * P * j : 2 * P * (j + 1), :].rearrange("(r a) k -> r a k", a=2)
+            rows = Wo[2 * P * j : 2 * P * (j + 1), :].rearrange("(a r) k -> r a k", a=2)
             if j in (0, 5):
                 for g in range(NG):
                     nc.sync.dma_start(out=wraw[j][:, :, g * 512 : (g + 1) * 512], in_=rows[:, :, g * 512 : (g + 1) * 512])
@@ -101,46 +101,42 @@ def tile_hierarchicalattention_pb_kernel(tc, ctx_heads, Wo, bo, features, ln_g, 
         def spread(out, v, c):
             nc.tensor.matmul(out=out, lhsT=ones[:], rhs=vz[v][:, c * CW : (c + 1) * CW], start=True, stop=True)
 
-        def spread_bo(c):
-            ps = work.tile([P, CW], F32, name="wk", tag="wk")
-            spread(ps[:], 0, c)
-            nc.scalar.copy(out=bo_bc[:, c * CW : (c + 1) * CW], in_=ps[:])
+        def spread_bo():
+            for c in range(NC):
+                ps = work.tile([P, CW], F32, name="wk", tag="wk")
+                spread(ps[:], 0, c)
+                nc.scalar.copy(out=bo_bc[:, c * CW : (c + 1) * CW], in_=ps[:])
 
-        spreads = [
-            [lambda: spread_bo(0), lambda: spread_bo(1)],
-            [lambda: spread_bo(2), lambda: spread(g_ps[:, 0:CW], 1, 0)],
-            [lambda: spread(g_ps[:, CW:CA], 1, 1), lambda: spread(b_ps[:, 0:CW], 2, 0)],
-            [lambda: spread(b_ps[:, CW:CA], 2, 1), lambda: spread(gb_ps[:, 0:CW], 1, 2)],
-            [lambda: spread(gb_ps[:, CW : 2 * CW], 2, 2)],
-        ]
+        def spread_g():
+            spread(g_ps[:, 0:CW], 1, 0)
+            spread(g_ps[:, CW:CA], 1, 1)
+
+        def spread_b():
+            spread(b_ps[:, 0:CW], 2, 0)
+            spread(b_ps[:, CW:CA], 2, 1)
+            spread(gb_ps[:, 0:CW], 1, 2)
+            spread(gb_ps[:, CW : 2 * CW], 2, 2)
 
         def add_bias(m):
-            for c in range(H // 256):
-                sl = slice(c * 256, (c + 1) * 256)
+            for sl in (slice(0, 2 * CW), slice(2 * CW, H)):
                 nc.gpsimd.tensor_tensor(out=yt[m][:, sl], in0=feat[m][:, sl], in1=bo_bc[:, sl], op=ALU.add)
 
-        def turn(blocks, on_vector, rows_interleaved):
+        def turn(blocks, on_vector):
             tp = work.tile([P, 2, 2, P], F32, name="wk", tag="wk")
             for a, (words, g) in enumerate(blocks):
                 for u in range(2):
                     nc.tensor.transpose(out=tp[:, a, u, :], in_=words[:, 256 * g + u : 256 * (g + 1) : 2], identity=ident[:])
             n = len(blocks)
-            grp = stage.tile([P, 2 * P, 4], BF16, name="grp", tag="grp", align_bytes=64)
-            if rows_interleaved:
-                dst = grp[:].bitcast(F32).rearrange("p (r a) u -> p r a u", a=2)
-                src = tp[:].rearrange("p a u r -> p r a u")
-            else:
-                dst = grp[:, 0 : n * P].bitcast(F32).rearrange("p (a r) u -> p a r u", a=n)
-                src = tp[:, 0:n].rearrange("p a u r -> p a r u")
+            grp = stage.tile([P, 2, P, 4], BF16, name="grp", tag="grp", align_bytes=64)
             if on_vector:
-                nc.vector.tensor_copy(out=dst, in_=src)
+                nc.vector.tensor_copy(out=grp[:, 0:n].bitcast(F32), in_=tp[:, 0:n].rearrange("p a u r -> p a r u"))
             else:
-                nc.scalar.copy(out=dst, in_=src)
+                nc.scalar.copy(out=grp[:, 0:n].bitcast(F32), in_=tp[:, 0:n].rearrange("p a u r -> p a r u"))
             return grp
 
         def turn_w(j):
             words = wraw[j][:].bitcast(F32)
-            return [turn([(words[:, 0, :], g), (words[:, 1, :], g)], g == 0, True) for g in range(NG)]
+            return [turn([(words[:, 0, :], g), (words[:, 1, :], g)], g == 0) for g in range(NG)]
 
         def quant_w(j, grps):
             n, a = j // 2, j % 2
@@ -148,23 +144,23 @@ def tile_hierarchicalattention_pb_kernel(tc, ctx_heads, Wo, bo, features, ln_g, 
                 nc.vector.quantize_mx(
                     out=wq[n][:, g, a * 256 : (a + 1) * 256].bitcast(FP8X4),
                     scales=ws[n][:, g, a * 256 : (a + 1) * 256],
-                    in_=grps[g][:].rearrange("p c t -> p (c t)"),
+                    in_=grps[g][:].rearrange("p a r t -> p (a r t)"),
                 )
 
         def turn_c(m):
             words = craw[m][:].bitcast(F32)
-            return [turn([(words, 0), (words, 1)], False, False), turn([(words, 2)], False, False)]
+            return [turn([(words, 0), (words, 1)], False), turn([(words, 2)], False)]
 
         def quant_c(m, grps):
             nc.vector.quantize_mx(
                 out=cq[m][:, 0:2, :].rearrange("p g s -> p (g s)").bitcast(FP8X4),
                 scales=cs[m][:, 0:2, :].rearrange("p g s -> p (g s)"),
-                in_=grps[0][:].rearrange("p c t -> p (c t)"),
+                in_=grps[0][:].rearrange("p a r t -> p (a r t)"),
             )
             nc.vector.quantize_mx(
                 out=cq[m][:, 2, :].bitcast(FP8X4),
                 scales=cs[m][:, 2, :],
-                in_=grps[1][:, 0:P].rearrange("p c t -> p (c t)"),
+                in_=grps[1][:, 0].rearrange("p r t -> p (r t)"),
             )
 
         accs = {}
@@ -221,14 +217,14 @@ def tile_hierarchicalattention_pb_kernel(tc, ctx_heads, Wo, bo, features, ln_g, 
 
         for j in range(5):
             grps = turn_w(j)
-            for f in spreads[j]:
-                f()
-            if j == 1:
+            if j == 0:
+                spread_bo()
                 for m in range(3):
                     add_bias(m)
             quant_w(j, grps)
         cgrp = {}
         cgrp[0] = turn_c(0)
+        spread_g()
         quant_c(0, cgrp[0])
         grps = turn_w(5)
         product(0, 0)
@@ -236,6 +232,7 @@ def tile_hierarchicalattention_pb_kernel(tc, ctx_heads, Wo, bo, features, ln_g, 
         cgrp[1] = turn_c(1)
         quant_w(5, grps)
         product(0, 2)
+        spread_b()
         residual(0, 0)
         residual(0, 1)
         quant_c(1, cgrp[1])

@@ -241,9 +241,12 @@ def tile_hierarchicalattention_pb_kernel(tc, ctx_heads, Wo, bo, features, ln_g, 
 
         for m in range(NT):
             last = m == NT - 1
-            nc.vector.tensor_scalar(
-                out=s1j[m][:], in0=s1[m][:], scalar1=-1.0 / H, scalar2=None, op0=ALU.mult, op1=ALU.add, accum_out=negmean[m][:]
-            )
+            if m == 0:
+                nc.vector.tensor_scalar(
+                    out=s1j[m][:], in0=s1[m][:], scalar1=-1.0 / H, scalar2=None, op0=ALU.mult, op1=ALU.add, accum_out=negmean[m][:]
+                )
+            else:
+                nc.scalar.activation(out=s1j[m][:], in_=s1[m][:], func=ACT.Copy, scale=-1.0 / H, accum_out=negmean[m][:])
             sq = stage.tile([P, H], BF16, name="sq", tag="sq", bufs=2)
             nc.scalar.activation(out=sq[:], in_=yt[m][:], func=ACT.Square, bias=negmean[m][:], scale=1.0, accum_out=m2[m][:])
             nc.scalar.activation(out=std[m][:], in_=m2[m][:], func=ACT.Sqrt, bias=eps[:], scale=1.0 / H)

@@ -80,11 +80,13 @@ def tile_hierarchicalattention_pb_kernel(tc, ctx_heads, Wo, bo, features, ln_g, 
         def load_f(m):
             nc.sync.dma_start(out=feat[m][:], in_=features[m])
 
-        for j in range(5):
+        for j in range(3):
             load_w(j)
+        load_f(0)
+        load_w(3)
+        load_w(4)
         load_c(0)
         load_w(5)
-        load_f(0)
         for m in range(1, NT):
             load_c(m)
             load_f(m)
@@ -94,7 +96,7 @@ def tile_hierarchicalattention_pb_kernel(tc, ctx_heads, Wo, bo, features, ln_g, 
             nc.vector.memset(vz[v][:].bitcast(I32), 0)
         make_identity(nc, ident[:])
         nc.gpsimd.memset(ones[:], 1.0)
-        nc.scalar.activation(out=warm[:], in_=eps[:], func=ACT.Sqrt)
+        nc.scalar.activation(out=warm[:], in_=eps[:], func=ACT.Abs_reciprocal_sqrt)
         for v, vec in enumerate((bo, ln_g, ln_b)):
             nc.scalar.dma_start(out=vz[v][0:1, :], in_=vec.rearrange("(o n) -> o n", o=1))
 
@@ -118,6 +120,7 @@ def tile_hierarchicalattention_pb_kernel(tc, ctx_heads, Wo, bo, features, ln_g, 
             spread(gb_ps[:, CW : 2 * CW], 2, 2)
 
         def add_bias(m):
+            nc.vector.tensor_copy(out=yt[m][:, 0:1], in_=eps[:])
             for sl in (slice(0, 2 * CW), slice(2 * CW, H)):
                 nc.gpsimd.tensor_tensor(out=yt[m][:, sl], in0=feat[m][:, sl], in1=bo_bc[:, sl], op=ALU.add)
 
@@ -136,7 +139,7 @@ def tile_hierarchicalattention_pb_kernel(tc, ctx_heads, Wo, bo, features, ln_g, 
 
         def turn_w(j):
             words = wraw[j][:].bitcast(F32)
-            return [turn([(words[:, 0, :], g), (words[:, 1, :], g)], g == 0) for g in range(NG)]
+            return [turn([(words[:, 0, :], g), (words[:, 1, :], g)], g == 0 and j < 3) for g in range(NG)]
 
         def quant_w(j, grps):
             n, a = j // 2, j % 2
@@ -194,14 +197,6 @@ def tile_hierarchicalattention_pb_kernel(tc, ctx_heads, Wo, bo, features, ln_g, 
         def norm_shift(m, sl, b_ap):
             nc.vector.scalar_tensor_tensor(out=ot[m][:, sl], in0=ot[m][:, sl], scalar=rstd[m][:], in1=b_ap, op0=ALU.mult, op1=ALU.add)
 
-        def finish_b(m):
-            if m < G_TILES:
-                nc.gpsimd.tensor_scalar(out=ot[m][:, B], in0=yt[m][:, B], scalar1=negmean[m][:], scalar2=rstd[m][:], op0=ALU.add, op1=ALU.mult)
-                nc.gpsimd.tensor_tensor(out=ot[m][:, B], in0=ot[m][:, B], in1=gb_sb[:, 0:CW], op=ALU.mult)
-                nc.gpsimd.tensor_tensor(out=ot[m][:, B], in0=ot[m][:, B], in1=gb_sb[:, CW : 2 * CW], op=ALU.add)
-            else:
-                norm_shift(m, B, gb_ps[:, CW : 2 * CW])
-
         owed = []
 
         def pay():
@@ -219,9 +214,9 @@ def tile_hierarchicalattention_pb_kernel(tc, ctx_heads, Wo, bo, features, ln_g, 
             grps = turn_w(j)
             if j == 0:
                 spread_bo()
-                for m in range(3):
-                    add_bias(m)
             quant_w(j, grps)
+            if j == 3:
+                nc.vector.tensor_tensor(out=yt[0][:], in0=feat[0][:], in1=bo_bc[:], op=ALU.add)
         cgrp = {}
         cgrp[0] = turn_c(0)
         spread_g()
@@ -236,6 +231,7 @@ def tile_hierarchicalattention_pb_kernel(tc, ctx_heads, Wo, bo, features, ln_g, 
         residual(0, 0)
         residual(0, 1)
         quant_c(1, cgrp[1])
+        add_bias(1)
         cgrp[2] = turn_c(2)
         residual(0, 2)
 
@@ -249,33 +245,27 @@ def tile_hierarchicalattention_pb_kernel(tc, ctx_heads, Wo, bo, features, ln_g, 
                 nc.scalar.activation(out=s1j[m][:], in_=s1[m][:], func=ACT.Copy, scale=-1.0 / H, accum_out=negmean[m][:])
             sq = stage.tile([P, H], BF16, name="sq", tag="sq", bufs=2)
             nc.scalar.activation(out=sq[:], in_=yt[m][:], func=ACT.Square, bias=negmean[m][:], scale=1.0, accum_out=m2[m][:])
-            nc.scalar.activation(out=std[m][:], in_=m2[m][:], func=ACT.Sqrt, bias=eps[:], scale=1.0 / H)
+            nc.scalar.activation(out=rstd[m][:], in_=m2[m][:], func=ACT.Abs_reciprocal_sqrt, bias=eps[:], scale=1.0 / H)
             if m > 0:
-                finish_b(m - 1)
+                norm_shift(m - 1, A, b_ps[:])
                 leave(m - 1, A)
-                leave(m - 1, B)
-            if m == 1:
-                add_bias(3)
             if not last:
                 for n in range(NC):
                     product(m + 1, n)
             if m + 3 < NT:
                 cgrp[m + 3] = turn_c(m + 3)
-            if 0 < m and not last:
-                residual(m + 1, 0)
             centre_scale(m, A, g_ps[:])
-            if m >= G_TILES:
-                centre_scale(m, B, gb_ps[:, 0:CW])
-            if m == 0:
+            centre_scale(m, B, gb_ps[:, 0:CW])
+            if m > 0:
+                norm_shift(m - 1, B, gb_ps[:, CW : 2 * CW])
+                leave(m - 1, B)
+            if not last:
                 residual(m + 1, 0)
-            if not last:
                 residual(m + 1, 1)
-            if m + 2 < NT:
-                quant_c(m + 2, cgrp[m + 2])
-            nc.vector.reciprocal(out=rstd[m][:], in_=std[m][:])
-            if not last:
+                if m + 2 < NT:
+                    quant_c(m + 2, cgrp[m + 2])
+                    add_bias(m + 2)
                 residual(m + 1, 2)
-                norm_shift(m, A, b_ps[:])
         m = NT - 1
         for c, b_ap in enumerate((b_ps[:, 0:CW], b_ps[:, CW:CA], gb_ps[:, CW : 2 * CW])):
             sl = slice(c * CW, (c + 1) * CW)

@@ -29,7 +29,7 @@ FLOPS = 2 * NT * P * K * H
 def tile_hierarchicalattention_pb_kernel(tc, ctx_heads, Wo, bo, features, ln_g, ln_b, out_0, out_1):
     nc = tc.nc
     CA = 2 * CW
-    G_TILES = 0
+    G_TILE = 2
     with ExitStack() as ctx:
         const = ctx.enter_context(tc.tile_pool(name="const", bufs=1))
         raw = ctx.enter_context(tc.tile_pool(name="raw", bufs=1))
@@ -191,6 +191,14 @@ def tile_hierarchicalattention_pb_kernel(tc, ctx_heads, Wo, bo, features, ln_g, 
         A = slice(0, CA)
         B = slice(CA, H)
 
+        nmr = keep.tile([P, 1], F32, name="nmr", tag="nmr")
+
+        def finish_on_gpsimd(m):
+            nc.scalar.activation(out=nmr[:], in_=negmean[m][:], func=ACT.Copy, scale=rstd[m][:])
+            nc.scalar.activation(out=ot[m][:, B], in_=yt[m][:, B], func=ACT.Identity, bias=nmr[:], scale=rstd[m][:])
+            nc.gpsimd.tensor_tensor(out=ot[m][:, B], in0=ot[m][:, B], in1=gb_sb[:, 0:CW], op=ALU.mult)
+            nc.gpsimd.tensor_tensor(out=ot[m][:, B], in0=ot[m][:, B], in1=gb_sb[:, CW : 2 * CW], op=ALU.add)
+
         def centre_scale(m, sl, g_ap):
             nc.vector.scalar_tensor_tensor(out=ot[m][:, sl], in0=yt[m][:, sl], scalar=negmean[m][:], in1=g_ap, op0=ALU.add, op1=ALU.mult)
 
@@ -228,6 +236,7 @@ def tile_hierarchicalattention_pb_kernel(tc, ctx_heads, Wo, bo, features, ln_g, 
         quant_w(5, grps)
         product(0, 2)
         spread_b()
+        nc.scalar.copy(out=gb_sb[:], in_=gb_ps[:])
         residual(0, 0)
         residual(0, 1)
         quant_c(1, cgrp[1])
@@ -246,18 +255,25 @@ def tile_hierarchicalattention_pb_kernel(tc, ctx_heads, Wo, bo, features, ln_g, 
             sq = stage.tile([P, H], BF16, name="sq", tag="sq", bufs=2)
             nc.scalar.activation(out=sq[:], in_=yt[m][:], func=ACT.Square, bias=negmean[m][:], scale=1.0, accum_out=m2[m][:])
             nc.scalar.activation(out=rstd[m][:], in_=m2[m][:], func=ACT.Abs_reciprocal_sqrt, bias=eps[:], scale=1.0 / H)
+            if m == G_TILE:
+                finish_on_gpsimd(m)
             if m > 0:
                 norm_shift(m - 1, A, b_ps[:])
-                leave(m - 1, A)
+                if last:
+                    nc.sync.dma_start(out=out_0[m - 1][:, A], in_=ot[m - 1][:, A])
+                else:
+                    leave(m - 1, A)
             if not last:
                 for n in range(NC):
                     product(m + 1, n)
             if m + 3 < NT:
                 cgrp[m + 3] = turn_c(m + 3)
             centre_scale(m, A, g_ps[:])
-            centre_scale(m, B, gb_ps[:, 0:CW])
+            if m != G_TILE:
+                centre_scale(m, B, gb_ps[:, 0:CW])
             if m > 0:
-                norm_shift(m - 1, B, gb_ps[:, CW : 2 * CW])
+                if m - 1 != G_TILE:
+                    norm_shift(m - 1, B, gb_ps[:, CW : 2 * CW])
                 leave(m - 1, B)
             if not last:
                 residual(m + 1, 0)
@@ -271,4 +287,6 @@ def tile_hierarchicalattention_pb_kernel(tc, ctx_heads, Wo, bo, features, ln_g, 
             sl = slice(c * CW, (c + 1) * CW)
             norm_shift(m, sl, b_ap)
             leave(m, sl)
+        nc.vector.tensor_scalar(out=o8[m - 1][:, A], in0=ot[m - 1][:, A], scalar1=Y_SCALE, scalar2=None, op0=ALU.mult, saturate=False)
+        owed.append((m - 1, A))
         pay()

@@ -68,8 +68,11 @@ def tile_hierarchicalattention_pb_kernel(tc, ctx_heads, Wo, bo, features, ln_g, 
 
         def load_w(j):
             rows = Wo[2 * P * j : 2 * P * (j + 1), :].rearrange("(a r) k -> r a k", a=2)
+            if j == 0:
+                for a in range(2):
+                    nc.sync.dma_start(out=wraw[j][:, a, 0:512], in_=rows[:, a, 0:512])
             if j in (0, 5):
-                for g in range(NG):
+                for g in range(1 if j == 0 else 0, NG):
                     nc.sync.dma_start(out=wraw[j][:, :, g * 512 : (g + 1) * 512], in_=rows[:, :, g * 512 : (g + 1) * 512])
             else:
                 nc.sync.dma_start(out=wraw[j][:], in_=rows)

@@ -281,10 +281,13 @@ def tile_hierarchicalattention_pb_kernel(tc, ctx_heads, Wo, bo, features, ln_g, 
             if not last:
                 residual(m + 1, 0)
                 residual(m + 1, 1)
+                if m == 0:
+                    residual(m + 1, 2)
                 if m + 2 < NT:
                     quant_c(m + 2, cgrp[m + 2])
                     add_bias(m + 2)
-                residual(m + 1, 2)
+                if m > 0:
+                    residual(m + 1, 2)
         m = NT - 1
         for c, b_ap in enumerate((b_ps[:, 0:CW], b_ps[:, CW:CA], gb_ps[:, CW : 2 * CW])):
             sl = slice(c * CW, (c + 1) * CW)

@@ -90,9 +90,12 @@ def tile_hierarchicalattention_pb_kernel(tc, ctx_heads, Wo, bo, features, ln_g, 
         load_w(4)
         load_c(0)
         load_w(5)
-        for m in range(1, NT):
-            load_c(m)
-            load_f(m)
+        load_f(1)
+        load_c(1)
+        load_c(2)
+        load_c(3)
+        load_f(2)
+        load_f(3)
 
         nc.gpsimd.memset(eps[:], LN_EPS)
         for v in range(3):
@@ -221,35 +224,53 @@ def tile_hierarchicalattention_pb_kernel(tc, ctx_heads, Wo, bo, features, ln_g, 
             pay()
             owed.append((m, sl))
 
-        for j in range(5):
-            grps = turn_w(j)
-            if j == 0:
-                spread_bo()
-            quant_w(j, grps)
-            if j == 3:
-                nc.vector.tensor_tensor(out=yt[0][:], in0=feat[0][:], in1=bo_bc[:], op=ALU.add)
-        cgrp = {}
-        cgrp[0] = turn_c(0)
-        spread_g()
-        quant_c(0, cgrp[0])
-        grps = turn_w(5)
-        product(0, 0)
-        product(0, 1)
-        cgrp[1] = turn_c(1)
-        quant_w(5, grps)
-        product(0, 2)
-        spread_b()
-        nc.scalar.copy(out=gb_sb[:], in_=gb_ps[:])
-        residual(0, 0)
-        residual(0, 1)
-        quant_c(1, cgrp[1])
-        add_bias(1)
-        cgrp[2] = turn_c(2)
-        residual(0, 2)
+        def turn_w1(j, g, on_vector):
+            words = wraw[j][:].bitcast(F32)
+            return turn([(words[:, 0, :], g), (words[:, 1, :], g)], on_vector)
 
-        for m in range(NT):
-            last = m == NT - 1
-            if m == 0:
+        def quant_w1(j, g, grp):
+            n, a = j // 2, j % 2
+            nc.vector.quantize_mx(
+                out=wq[n][:, g, a * 256 : (a + 1) * 256].bitcast(FP8X4),
+                scales=ws[n][:, g, a * 256 : (a + 1) * 256],
+                in_=grp[:].rearrange("p a r t -> p (a r t)"),
+            )
+
+        def open_acc(m, n):
+            accs[(m, n)] = work.tile([P, CW], F32, name="wk", tag="wk")
+
+        def mx_pass(m, n, g):
+            nc.tensor.matmul_mx(
+                out=accs[(m, n)][:],
+                lhsT=cq[m][:, g, :].bitcast(FP8X4),
+                lhsT_scale=cs[m][:, g, :],
+                rhs=wq[n][:, g, :].bitcast(FP8X4),
+                rhs_scale=ws[n][:, g, :],
+                start=(g == 0),
+                stop=(g == NG - 1),
+            )
+
+        def hold_gpsimd(m):
+            nc.vector.tensor_copy(out=yt[m][:, 0:1], in_=eps[:])
+
+        def bias_on_gpsimd(m, sl):
+            nc.gpsimd.tensor_tensor(out=yt[m][:, sl], in0=feat[m][:, sl], in1=bo_bc[:, sl], op=ALU.add)
+
+        nmrs = [keep.tile([P, 1], F32, name="nmr%d" % m, tag="nmr%d" % m) for m in range(NT)]
+        def finish_chunk(m):
+            nc.scalar.activation(out=nmrs[m][:], in_=negmean[m][:], func=ACT.Copy, scale=rstd[m][:])
+            nc.scalar.activation(out=ot[m][:, B], in_=yt[m][:, B], func=ACT.Identity, bias=nmrs[m][:], scale=rstd[m][:])
+            nc.gpsimd.tensor_tensor(out=ot[m][:, B], in0=ot[m][:, B], in1=gb_sb[:, 0:CW], op=ALU.mult)
+            nc.gpsimd.tensor_tensor(out=ot[m][:, B], in0=ot[m][:, B], in1=gb_sb[:, CW : 2 * CW], op=ALU.add)
+
+        def spread_for_gpsimd():
+            ps = work.tile([P, 2 * CW], BF16, name="wk", tag="wk")
+            spread(ps[:, 0:CW], 1, 2)
+            spread(ps[:, CW : 2 * CW], 2, 2)
+            nc.scalar.copy(out=gb_sb[:], in_=ps[:])
+
+        def stats(m, on_vector):
+            if on_vector:
                 nc.vector.tensor_scalar(
                     out=s1j[m][:], in0=s1[m][:], scalar1=-1.0 / H, scalar2=None, op0=ALU.mult, op1=ALU.add, accum_out=negmean[m][:]
                 )
@@ -258,41 +279,84 @@ def tile_hierarchicalattention_pb_kernel(tc, ctx_heads, Wo, bo, features, ln_g, 
             sq = stage.tile([P, H], BF16, name="sq", tag="sq", bufs=2)
             nc.scalar.activation(out=sq[:], in_=yt[m][:], func=ACT.Square, bias=negmean[m][:], scale=1.0, accum_out=m2[m][:])
             nc.scalar.activation(out=rstd[m][:], in_=m2[m][:], func=ACT.Abs_reciprocal_sqrt, bias=eps[:], scale=1.0 / H)
-            if m == G_TILE:
-                finish_on_gpsimd(m)
-            if m > 0:
-                norm_shift(m - 1, A, b_ps[:])
-                if last:
-                    nc.sync.dma_start(out=out_0[m - 1][:, A], in_=ot[m - 1][:, A])
-                else:
-                    leave(m - 1, A)
-            if not last:
-                for n in range(NC):
-                    product(m + 1, n)
-            if m + 3 < NT:
-                cgrp[m + 3] = turn_c(m + 3)
-            centre_scale(m, A, g_ps[:])
-            if m != G_TILE:
-                centre_scale(m, B, gb_ps[:, 0:CW])
-            if m > 0:
-                if m - 1 != G_TILE:
-                    norm_shift(m - 1, B, gb_ps[:, CW : 2 * CW])
-                leave(m - 1, B)
-            if not last:
-                residual(m + 1, 0)
-                residual(m + 1, 1)
-                if m == 0:
-                    residual(m + 1, 2)
-                if m + 2 < NT:
-                    quant_c(m + 2, cgrp[m + 2])
-                    add_bias(m + 2)
-                if m > 0:
-                    residual(m + 1, 2)
+
+        cgrp = {}
+        for j in range(5):
+            grps = turn_w(j)
+            if j == 0:
+                spread_bo()
+            if j == 2:
+                spread_g()
+            quant_w(j, grps)
+            if j == 2:
+                nc.vector.tensor_tensor(out=yt[0][:], in0=feat[0][:], in1=bo_bc[:], op=ALU.add)
+        cgrp[0] = turn_c(0)
+        grps = [turn_w1(5, g, False) for g in range(NG)]
+        quant_c(0, cgrp[0])
+        for g in range(NG):
+            quant_w1(5, g, grps[g])
+        hold_gpsimd(1)
+        bias_on_gpsimd(1, A)
+        for n in range(NC):
+            product(0, n)
+        residual(0, 0)
+        residual(0, 1)
+        cgrp[1] = turn_c(1)
+        residual(0, 2)
+        spread_b()
+
+        stats(0, True)
+        cgrp[2] = turn_c(2)
+        cgrp[3] = turn_c(3)
+        centre_scale(0, A, g_ps[:])
+        centre_scale(0, B, gb_ps[:, 0:CW])
+        quant_c(1, cgrp[1])
+        for n in range(NC):
+            product(1, n)
+        nc.vector.tensor_tensor(out=yt[1][:, B], in0=feat[1][:, B], in1=bo_bc[:, B], op=ALU.add)
+        norm_shift(0, A, b_ps[:])
+        leave(0, A)
+        quant_c(2, cgrp[2])
+        quant_c(3, cgrp[3])
+        hold_gpsimd(2)
+        for m in (2, 3):
+            bias_on_gpsimd(m, A)
+            bias_on_gpsimd(m, B)
+        spread_for_gpsimd()
+        for n in range(NC):
+            product(2, n)
+        for n in range(NC):
+            residual(1, n)
+        stats(1, False)
+        norm_shift(0, B, gb_ps[:, CW : 2 * CW])
+        leave(0, B)
+        finish_chunk(1)
+        centre_scale(1, A, g_ps[:])
+        for n in range(NC):
+            product(3, n)
+        for n in range(NC):
+            residual(2, n)
+        stats(2, False)
+        finish_chunk(2)
+        norm_shift(1, A, b_ps[:])
+        leave(1, A)
+        centre_scale(2, A, g_ps[:])
+        for n in range(NC):
+            residual(3, n)
+        stats(3, False)
+        leave(1, B)
+        norm_shift(2, A, b_ps[:])
+        leave(2, A)
+        centre_scale(3, A, g_ps[:])
+        centre_scale(3, B, gb_ps[:, 0:CW])
         m = NT - 1
-        for c, b_ap in enumerate((b_ps[:, 0:CW], b_ps[:, CW:CA], gb_ps[:, CW : 2 * CW])):
-            sl = slice(c * CW, (c + 1) * CW)
-            norm_shift(m, sl, b_ap)
-            leave(m, sl)
-        nc.vector.tensor_scalar(out=o8[m - 1][:, A], in0=ot[m - 1][:, A], scalar1=Y_SCALE, scalar2=None, op0=ALU.mult, saturate=False)
-        owed.append((m - 1, A))
+        norm_shift(m, slice(0, CW), b_ps[:, 0:CW])
+        leave(m, slice(0, CW))
+        leave(2, B)
+        norm_shift(m, slice(CW, CA), b_ps[:, CW:CA])
+        nc.sync.dma_start(out=out_0[m][:, CW:CA], in_=ot[m][:, CW:CA])
+        norm_shift(m, B, gb_ps[:, CW : 2 * CW])
+        nc.sync.dma_start(out=out_0[m][:, B], in_=ot[m][:, B])
         pay()
+        nc.vector.tensor_scalar(out=o8[m][:, CW:H], in0=ot[m][:, CW:H], scalar1=Y_SCALE, scalar2=None, op0=ALU.mult, saturate=False)
+        nc.sync.dma_start(out=out_1[m][:, CW:H], in_=o8[m][:, CW:H].bitcast(U8))

@@ -337,22 +337,23 @@ def tile_hierarchicalattention_pb_kernel(tc, ctx_heads, Wo, bo, features, ln_g, 
         for n in range(NC):
             residual(2, n)
         stats(2, False)
-        finish_chunk(2)
         norm_shift(1, A, b_ps[:])
         leave(1, A)
         centre_scale(2, A, g_ps[:])
+        centre_scale(2, B, gb_ps[:, 0:CW])
         for n in range(NC):
             residual(3, n)
         stats(3, False)
         leave(1, B)
         norm_shift(2, A, b_ps[:])
         leave(2, A)
+        norm_shift(2, B, gb_ps[:, CW : 2 * CW])
+        leave(2, B)
         centre_scale(3, A, g_ps[:])
         centre_scale(3, B, gb_ps[:, 0:CW])
         m = NT - 1
         norm_shift(m, slice(0, CW), b_ps[:, 0:CW])
         leave(m, slice(0, CW))
-        leave(2, B)
         norm_shift(m, slice(CW, CA), b_ps[:, CW:CA])
         nc.sync.dma_start(out=out_0[m][:, CW:CA], in_=ot[m][:, CW:CA])
         norm_shift(m, B, gb_ps[:, CW : 2 * CW])

@@ -67,7 +67,7 @@ def tile_hierarchicalattention_pb_kernel(tc, ctx_heads, Wo, bo, features, ln_g, 
         gb_ps = gbp.tile([P, 2 * CW], BF16, name="gb_ps", tag="gb_ps")
 
         def load_w(j):
-            rows = Wo[2 * P * j : 2 * P * (j + 1), :].rearrange("(a r) k -> r a k", a=2)
+            rows = Wo[2 * P * j : 2 * P * (j + 1), :].rearrange("(r a) k -> r a k", a=2)
             if j == 0:
                 for a in range(2):
                     nc.sync.dma_start(out=wraw[j][:, a, 0:512], in_=rows[:, a, 0:512])
@@ -130,22 +130,28 @@ def tile_hierarchicalattention_pb_kernel(tc, ctx_heads, Wo, bo, features, ln_g, 
             for sl in (slice(0, 2 * CW), slice(2 * CW, H)):
                 nc.gpsimd.tensor_tensor(out=yt[m][:, sl], in0=feat[m][:, sl], in1=bo_bc[:, sl], op=ALU.add)
 
-        def turn(blocks, on_vector):
+        def turn(blocks, on_vector, woven=False):
             tp = work.tile([P, 2, 2, P], F32, name="wk", tag="wk")
             for a, (words, g) in enumerate(blocks):
                 for u in range(2):
                     nc.tensor.transpose(out=tp[:, a, u, :], in_=words[:, 256 * g + u : 256 * (g + 1) : 2], identity=ident[:])
             n = len(blocks)
             grp = stage.tile([P, 2, P, 4], BF16, name="grp", tag="grp", align_bytes=64)
-            if on_vector:
-                nc.vector.tensor_copy(out=grp[:, 0:n].bitcast(F32), in_=tp[:, 0:n].rearrange("p a u r -> p a r u"))
+            if woven:
+                dst = grp[:].rearrange("p a r t -> p (a r t)").bitcast(F32).rearrange("p (r a u) -> p r a u", a=2, u=2)
+                src = tp[:].rearrange("p a u r -> p r a u")
             else:
-                nc.scalar.copy(out=grp[:, 0:n].bitcast(F32), in_=tp[:, 0:n].rearrange("p a u r -> p a r u"))
+                dst = grp[:, 0:n].bitcast(F32)
+                src = tp[:, 0:n].rearrange("p a u r -> p a r u")
+            if on_vector:
+                nc.vector.tensor_copy(out=dst, in_=src)
+            else:
+                nc.scalar.copy(out=dst, in_=src)
             return grp
 
         def turn_w(j):
             words = wraw[j][:].bitcast(F32)
-            return [turn([(words[:, 0, :], g), (words[:, 1, :], g)], g == 0 and j < 3) for g in range(NG)]
+            return [turn([(words[:, 0, :], g), (words[:, 1, :], g)], g == 0 and j < 3, True) for g in range(NG)]
 
         def quant_w(j, grps):
             n, a = j // 2, j % 2
@@ -226,7 +232,7 @@ def tile_hierarchicalattention_pb_kernel(tc, ctx_heads, Wo, bo, features, ln_g, 
 
         def turn_w1(j, g, on_vector):
             words = wraw[j][:].bitcast(F32)
-            return turn([(words[:, 0, :], g), (words[:, 1, :], g)], on_vector)
+            return turn([(words[:, 0, :], g), (words[:, 1, :], g)], on_vector, True)
 
         def quant_w1(j, g, grp):
             n, a = j // 2, j % 2
@@ -288,8 +294,9 @@ def tile_hierarchicalattention_pb_kernel(tc, ctx_heads, Wo, bo, features, ln_g, 
             if j == 2:
                 spread_g()
             quant_w(j, grps)
-            if j == 2:
-                nc.vector.tensor_tensor(out=yt[0][:], in0=feat[0][:], in1=bo_bc[:], op=ALU.add)
+            if j >= 2:
+                sl = slice((j - 2) * CW, (j - 1) * CW)
+                nc.vector.tensor_tensor(out=yt[0][:, sl], in0=feat[0][:, sl], in1=bo_bc[:, sl], op=ALU.add)
         cgrp[0] = turn_c(0)
         grps = [turn_w1(5, g, False) for g in range(NG)]
         quant_c(0, cgrp[0])

@@ -68,11 +68,18 @@ def tile_hierarchicalattention_pb_kernel(tc, ctx_heads, Wo, bo, features, ln_g, 
 
         def load_w(j):
             rows = Wo[2 * P * j : 2 * P * (j + 1), :].rearrange("(r a) k -> r a k", a=2)
+            if j == 5:
+                rows = Wo[2 * P * j : 2 * P * (j + 1), :].rearrange("(a r) k -> r a k", a=2)
+                for g in range(NG - 1):
+                    nc.sync.dma_start(out=wraw[j][:, :, g * 512 : (g + 1) * 512], in_=rows[:, :, g * 512 : (g + 1) * 512])
+                for a in range(2):
+                    nc.sync.dma_start(out=wraw[j][:, a, 1024:1536], in_=rows[:, a, 1024:1536])
+                return
             if j == 0:
                 for a in range(2):
                     nc.sync.dma_start(out=wraw[j][:, a, 0:512], in_=rows[:, a, 0:512])
-            if j in (0, 5):
-                for g in range(1 if j == 0 else 0, NG):
+            if j == 0:
+                for g in range(1, NG):
                     nc.sync.dma_start(out=wraw[j][:, :, g * 512 : (g + 1) * 512], in_=rows[:, :, g * 512 : (g + 1) * 512])
             else:
                 nc.sync.dma_start(out=wraw[j][:], in_=rows)
@@ -232,7 +239,7 @@ def tile_hierarchicalattention_pb_kernel(tc, ctx_heads, Wo, bo, features, ln_g, 
 
         def turn_w1(j, g, on_vector):
             words = wraw[j][:].bitcast(F32)
-            return turn([(words[:, 0, :], g), (words[:, 1, :], g)], on_vector, True)
+            return turn([(words[:, 0, :], g), (words[:, 1, :], g)], on_vector)
 
         def quant_w1(j, g, grp):
             n, a = j // 2, j % 2
@@ -298,10 +305,18 @@ def tile_hierarchicalattention_pb_kernel(tc, ctx_heads, Wo, bo, features, ln_g, 
                 sl = slice((j - 2) * CW, (j - 1) * CW)
                 nc.vector.tensor_tensor(out=yt[0][:, sl], in0=feat[0][:, sl], in1=bo_bc[:, sl], op=ALU.add)
         cgrp[0] = turn_c(0)
-        grps = [turn_w1(5, g, False) for g in range(NG)]
+        grps = [turn_w1(5, g, False) for g in range(NG - 1)]
+        words5 = wraw[5][:].bitcast(F32)
+        halves = [turn([(words5[:, a, :], NG - 1)], False) for a in range(2)]
         quant_c(0, cgrp[0])
-        for g in range(NG):
+        for g in range(NG - 1):
             quant_w1(5, g, grps[g])
+        for a in range(2):
+            nc.vector.quantize_mx(
+                out=wq[2][:, NG - 1, 256 + a * P : 256 + (a + 1) * P].bitcast(FP8X4),
+                scales=ws[2][:, NG - 1, 256 + a * P : 256 + (a + 1) * P],
+                in_=halves[a][:, 0].rearrange("p r t -> p (r t)"),
+            )
         hold_gpsimd(1)
         bias_on_gpsimd(1, A)
         for n in range(NC):

@@ -282,6 +282,34 @@ def tile_hierarchicalattention_pb_kernel(tc, ctx_heads, Wo, bo, features, ln_g, 
             spread(ps[:, CW : 2 * CW], 2, 2)
             nc.scalar.copy(out=gb_sb[:], in_=ps[:])
 
+        negc = [keep.tile([P, 1], F32, name="negc%d" % m, tag="negc%d" % m) for m in range(NT)]
+        q2 = [keep.tile([P, NC], F32, name="q2%d" % m, tag="q2%d" % m) for m in range(NT)]
+        q2j = [keep.tile([P, NC], F32, name="q2j%d" % m, tag="q2j%d" % m) for m in range(NT)]
+        d2 = [keep.tile([P, 1], F32, name="d2%d" % m, tag="d2%d" % m) for m in range(NT)]
+        ee = [keep.tile([P, 1], F32, name="ee%d" % m, tag="ee%d" % m) for m in range(NT)]
+
+        def pivot(m):
+            nc.scalar.activation(out=negc[m][:], in_=s1[m][:, 0:1], func=ACT.Copy, scale=-1.0 / CW)
+
+        def square(m, n):
+            sl = slice(n * CW, (n + 1) * CW)
+            sq = stage.tile([P, CW], BF16, name="sq", tag="sq", bufs=2)
+            nc.scalar.activation(out=sq[:], in_=yt[m][:, sl], func=ACT.Square, bias=negc[m][:], scale=1.0, accum_out=q2[m][:, n : n + 1])
+
+        def mean_of(m, on_vector):
+            if on_vector:
+                nc.vector.tensor_scalar(
+                    out=s1j[m][:], in0=s1[m][:], scalar1=-1.0 / H, scalar2=None, op0=ALU.mult, op1=ALU.add, accum_out=negmean[m][:]
+                )
+            else:
+                nc.scalar.activation(out=s1j[m][:], in_=s1[m][:], func=ACT.Copy, scale=-1.0 / H, accum_out=negmean[m][:])
+
+        def spread_of(m):
+            nc.scalar.activation(out=d2[m][:], in_=negmean[m][:], func=ACT.Square, bias=negc[m][:], scale=-1.0)
+            nc.scalar.activation(out=q2j[m][:], in_=q2[m][:], func=ACT.Copy, scale=1.0 / H, accum_out=m2[m][:])
+            nc.scalar.activation(out=ee[m][:], in_=d2[m][:], func=ACT.Copy, scale=-1.0, bias=LN_EPS)
+            nc.scalar.activation(out=rstd[m][:], in_=m2[m][:], func=ACT.Abs_reciprocal_sqrt, bias=ee[m][:], scale=1.0)
+
         def stats(m, on_vector):
             if on_vector:
                 nc.vector.tensor_scalar(
@@ -319,23 +347,29 @@ def tile_hierarchicalattention_pb_kernel(tc, ctx_heads, Wo, bo, features, ln_g, 
             )
         hold_gpsimd(1)
         bias_on_gpsimd(1, A)
+        bias_on_gpsimd(1, B)
         for n in range(NC):
             product(0, n)
         residual(0, 0)
+        pivot(0)
+        square(0, 0)
         residual(0, 1)
+        square(0, 1)
         cgrp[1] = turn_c(1)
         residual(0, 2)
         spread_b()
 
-        stats(0, True)
+        mean_of(0, True)
+        square(0, 2)
+        spread_of(0)
         cgrp[2] = turn_c(2)
         cgrp[3] = turn_c(3)
         centre_scale(0, A, g_ps[:])
         centre_scale(0, B, gb_ps[:, 0:CW])
+        spread_for_gpsimd()
         quant_c(1, cgrp[1])
         for n in range(NC):
             product(1, n)
-        nc.vector.tensor_tensor(out=yt[1][:, B], in0=feat[1][:, B], in1=bo_bc[:, B], op=ALU.add)
         norm_shift(0, A, b_ps[:])
         leave(0, A)
         quant_c(2, cgrp[2])
@@ -344,7 +378,6 @@ def tile_hierarchicalattention_pb_kernel(tc, ctx_heads, Wo, bo, features, ln_g, 
         for m in (2, 3):
             bias_on_gpsimd(m, A)
             bias_on_gpsimd(m, B)
-        spread_for_gpsimd()
         for n in range(NC):
             product(2, n)
         for n in range(NC):

@@ -333,7 +333,10 @@ def tile_hierarchicalattention_pb_kernel(tc, ctx_heads, Wo, bo, features, ln_g, 
                 sl = slice((j - 2) * CW, (j - 1) * CW)
                 nc.vector.tensor_tensor(out=yt[0][:, sl], in0=feat[0][:, sl], in1=bo_bc[:, sl], op=ALU.add)
         cgrp[0] = turn_c(0)
-        grps = [turn_w1(5, g, False) for g in range(NG - 1)]
+        grps = []
+        for g in range(NG - 1):
+            grps.append(turn_w1(5, g, False))
+            spread(gb_ps[:, g * CW : (g + 1) * CW], 1 + g, 2)
         words5 = wraw[5][:].bitcast(F32)
         halves = [turn([(words5[:, a, :], NG - 1)], False) for a in range(2)]
         quant_c(0, cgrp[0])
@@ -357,7 +360,8 @@ def tile_hierarchicalattention_pb_kernel(tc, ctx_heads, Wo, bo, features, ln_g, 
         square(0, 1)
         cgrp[1] = turn_c(1)
         residual(0, 2)
-        spread_b()
+        spread(b_ps[:, 0:CW], 2, 0)
+        spread(b_ps[:, CW:CA], 2, 1)
 
         mean_of(0, True)
         square(0, 2)
@@ -396,6 +400,7 @@ def tile_hierarchicalattention_pb_kernel(tc, ctx_heads, Wo, bo, features, ln_g, 
         leave(1, A)
         centre_scale(2, A, g_ps[:])
         centre_scale(2, B, gb_ps[:, 0:CW])
+        pay()
         for n in range(NC):
             residual(3, n)
         stats(3, False)

from contextlib import ExitStack

import concourse.mybir as mybir
from concourse.masks import make_identity

F32 = mybir.dt.float32
BF16 = mybir.dt.bfloat16
U32 = mybir.dt.uint32
U8 = mybir.dt.uint8
I32 = mybir.dt.int32
FP8X4 = mybir.dt.float8_e4m3fn_x4
FP8 = mybir.dt.float8_e4m3fn
ALU = mybir.AluOpType
ACT = mybir.ActivationFunctionType

P = 128
NT = 4
K = 1536
H = 1536
NG = 3
NC = 3
CW = 512
LN_EPS = 1e-5
Y_SCALE = 210.0

FLOPS = 2 * NT * P * K * H


def tile_hierarchicalattention_pb_kernel(tc, ctx_heads, Wo, bo, features, ln_g, ln_b, out_0, out_1):
    nc = tc.nc
    CA = 2 * CW
    G_TILE = 2
    with ExitStack() as ctx:
        const = ctx.enter_context(tc.tile_pool(name="const", bufs=1))
        raw = ctx.enter_context(tc.tile_pool(name="raw", bufs=1))
        keep = ctx.enter_context(tc.tile_pool(name="keep", bufs=1))
        stage = ctx.enter_context(tc.tile_pool(name="stage", bufs=6))
        work = ctx.enter_context(tc.psum_pool(name="work", bufs=5))
        gbp = ctx.enter_context(tc.psum_pool(name="gbp", bufs=1))
        ctx.enter_context(tc.manual_schedule())

        wraw = [raw.tile([P, 2, K], BF16, name="wraw%d" % j, tag="wraw%d" % j) for j in range(6)]
        craw = [raw.tile([P, K], BF16, name="craw%d" % m, tag="craw%d" % m) for m in range(NT)]
        feat = [raw.tile([P, H], BF16, name="feat%d" % m, tag="feat%d" % m) for m in range(NT)]
        wq = [keep.tile([P, NG, CW], U32, name="wq%d" % n, tag="wq%d" % n, align_bytes=64) for n in range(NC)]
        ws = [keep.tile([P, NG, CW], U8, name="ws%d" % n, tag="ws%d" % n, align_bytes=64) for n in range(NC)]
        cq = [keep.tile([P, NG, P], U32, name="cq%d" % m, tag="cq%d" % m, align_bytes=64) for m in range(NT)]
        cs = [keep.tile([P, NG, P], U8, name="cs%d" % m, tag="cs%d" % m, align_bytes=64) for m in range(NT)]
        yt = [keep.tile([P, H], F32, name="yt%d" % m, tag="yt%d" % m) for m in range(NT)]
        ot = [keep.tile([P, H], F32, name="ot%d" % m, tag="ot%d" % m) for m in range(NT)]
        o8 = [keep.tile([P, H], FP8, name="o8%d" % m, tag="o8%d" % m) for m in range(NT)]
        s1 = [keep.tile([P, NC], F32, name="s1%d" % m, tag="s1%d" % m) for m in range(NT)]
        s1j = [keep.tile([P, NC], F32, name="s1j%d" % m, tag="s1j%d" % m) for m in range(NT)]
        negmean = [keep.tile([P, 1], F32, name="nm%d" % m, tag="nm%d" % m) for m in range(NT)]
        m2 = [keep.tile([P, 1], F32, name="m2%d" % m, tag="m2%d" % m) for m in range(NT)]
        std = [keep.tile([P, 1], F32, name="sd%d" % m, tag="sd%d" % m) for m in range(NT)]
        rstd = [keep.tile([P, 1], F32, name="rs%d" % m, tag="rs%d" % m) for m in range(NT)]
        ident = const.tile([P, P], F32, name="ident", tag="ident")
        ones = const.tile([P, P], BF16, name="ones", tag="ones")
        eps = const.tile([P, 1], F32, name="eps", tag="eps")
        warm = const.tile([P, 1], F32, name="warm", tag="warm")
        vz = [const.tile([P, H], BF16, name="vz%d" % v, tag="vz%d" % v) for v in range(3)]
        bo_bc = const.tile([P, H], BF16, name="bo_bc", tag="bo_bc")
        gb_sb = const.tile([P, 2 * CW], BF16, name="gb_sb", tag="gb_sb")
        g_ps = gbp.tile([P, CA], BF16, name="g_ps", tag="g_ps")
        b_ps = gbp.tile([P, CA], BF16, name="b_ps", tag="b_ps")
        gb_ps = gbp.tile([P, 2 * CW], BF16, name="gb_ps", tag="gb_ps")

        def load_w(j):
            rows = Wo[2 * P * j : 2 * P * (j + 1), :].rearrange("(r a) k -> r a k", a=2)
            if j == 5:
                rows = Wo[2 * P * j : 2 * P * (j + 1), :].rearrange("(a r) k -> r a k", a=2)
                for g in range(NG - 1):
                    nc.sync.dma_start(out=wraw[j][:, :, g * 512 : (g + 1) * 512], in_=rows[:, :, g * 512 : (g + 1) * 512])
                for a in range(2):
                    nc.sync.dma_start(out=wraw[j][:, a, 1024:1536], in_=rows[:, a, 1024:1536])
                return
            if j == 0:
                for a in range(2):
                    nc.sync.dma_start(out=wraw[j][:, a, 0:512], in_=rows[:, a, 0:512])
            if j == 0:
                for g in range(1, NG):
                    nc.sync.dma_start(out=wraw[j][:, :, g * 512 : (g + 1) * 512], in_=rows[:, :, g * 512 : (g + 1) * 512])
            else:
                nc.sync.dma_start(out=wraw[j][:], in_=rows)

        def load_c(m):
            nc.sync.dma_start(out=craw[m][:].rearrange("s (h d) -> s h d", d=P), in_=ctx_heads[m].rearrange("h s d -> s h d"))

        def load_f(m):
            nc.sync.dma_start(out=feat[m][:], in_=features[m])

        for j in range(3):
            load_w(j)
        load_f(0)
        load_w(3)
        load_w(4)
        load_c(0)
        load_w(5)
        load_f(1)
        load_c(1)
        load_c(2)
        load_c(3)
        load_f(2)
        load_f(3)

        nc.gpsimd.memset(eps[:], LN_EPS)
        for v in range(3):
            nc.vector.memset(vz[v][:].bitcast(I32), 0)
        make_identity(nc, ident[:])
        nc.gpsimd.memset(ones[:], 1.0)
        nc.scalar.activation(out=warm[:], in_=eps[:], func=ACT.Abs_reciprocal_sqrt)
        for v, vec in enumerate((bo, ln_g, ln_b)):
            nc.scalar.dma_start(out=vz[v][0:1, :], in_=vec.rearrange("(o n) -> o n", o=1))

        def spread(out, v, c):
            nc.tensor.matmul(out=out, lhsT=ones[:], rhs=vz[v][:, c * CW : (c + 1) * CW], start=True, stop=True)

        def spread_bo():
            for c in range(NC):
                ps = work.tile([P, CW], F32, name="wk", tag="wk")
                spread(ps[:], 0, c)
                nc.scalar.copy(out=bo_bc[:, c * CW : (c + 1) * CW], in_=ps[:])

        def spread_g():
            spread(g_ps[:, 0:CW], 1, 0)
            spread(g_ps[:, CW:CA], 1, 1)

        def spread_b():
            spread(b_ps[:, 0:CW], 2, 0)
            spread(b_ps[:, CW:CA], 2, 1)
            spread(gb_ps[:, 0:CW], 1, 2)
            spread(gb_ps[:, CW : 2 * CW], 2, 2)

        def add_bias(m):
            nc.vector.tensor_copy(out=yt[m][:, 0:1], in_=eps[:])
            for sl in (slice(0, 2 * CW), slice(2 * CW, H)):
                nc.gpsimd.tensor_tensor(out=yt[m][:, sl], in0=feat[m][:, sl], in1=bo_bc[:, sl], op=ALU.add)

        def turn(blocks, on_vector, woven=False):
            tp = work.tile([P, 2, 2, P], F32, name="wk", tag="wk")
            for a, (words, g) in enumerate(blocks):
                for u in range(2):
                    nc.tensor.transpose(out=tp[:, a, u, :], in_=words[:, 256 * g + u : 256 * (g + 1) : 2], identity=ident[:])
            n = len(blocks)
            grp = stage.tile([P, 2, P, 4], BF16, name="grp", tag="grp", align_bytes=64)
            if woven:
                dst = grp[:].rearrange("p a r t -> p (a r t)").bitcast(F32).rearrange("p (r a u) -> p r a u", a=2, u=2)
                src = tp[:].rearrange("p a u r -> p r a u")
            else:
                dst = grp[:, 0:n].bitcast(F32)
                src = tp[:, 0:n].rearrange("p a u r -> p a r u")
            if on_vector:
                nc.vector.tensor_copy(out=dst, in_=src)
            else:
                nc.scalar.copy(out=dst, in_=src)
            return grp

        def turn_w(j):
            words = wraw[j][:].bitcast(F32)
            return [turn([(words[:, 0, :], g), (words[:, 1, :], g)], g == 0 and j < 3, True) for g in range(NG)]

        def quant_w(j, grps):
            n, a = j // 2, j % 2
            for g in range(NG):
                nc.vector.quantize_mx(
                    out=wq[n][:, g, a * 256 : (a + 1) * 256].bitcast(FP8X4),
                    scales=ws[n][:, g, a * 256 : (a + 1) * 256],
                    in_=grps[g][:].rearrange("p a r t -> p (a r t)"),
                )

        def turn_c(m):
            words = craw[m][:].bitcast(F32)
            return [turn([(words, 0), (words, 1)], False), turn([(words, 2)], False)]

        def quant_c(m, grps):
            nc.vector.quantize_mx(
                out=cq[m][:, 0:2, :].rearrange("p g s -> p (g s)").bitcast(FP8X4),
                scales=cs[m][:, 0:2, :].rearrange("p g s -> p (g s)"),
                in_=grps[0][:].rearrange("p a r t -> p (a r t)"),
            )
            nc.vector.quantize_mx(
                out=cq[m][:, 2, :].bitcast(FP8X4),
                scales=cs[m][:, 2, :],
                in_=grps[1][:, 0].rearrange("p r t -> p (r t)"),
            )

        accs = {}

        def product(m, n):
            acc = work.tile([P, CW], F32, name="wk", tag="wk")
            for g in range(NG):
                nc.tensor.matmul_mx(
                    out=acc[:],
                    lhsT=cq[m][:, g, :].bitcast(FP8X4),
                    lhsT_scale=cs[m][:, g, :],
                    rhs=wq[n][:, g, :].bitcast(FP8X4),
                    rhs_scale=ws[n][:, g, :],
                    start=(g == 0),
                    stop=(g == NG - 1),
                )
            accs[(m, n)] = acc

        def residual(m, n):
            sl = slice(n * CW, (n + 1) * CW)
            nc.vector.scalar_tensor_tensor(
                out=yt[m][:, sl], in0=accs[(m, n)][:], scalar=1.0, in1=yt[m][:, sl], op0=ALU.mult, op1=ALU.add, accum_out=s1[m][:, n : n + 1]
            )

        A = slice(0, CA)
        B = slice(CA, H)

        nmr = keep.tile([P, 1], F32, name="nmr", tag="nmr")

        def finish_on_gpsimd(m):
            nc.scalar.activation(out=nmr[:], in_=negmean[m][:], func=ACT.Copy, scale=rstd[m][:])
            nc.scalar.activation(out=ot[m][:, B], in_=yt[m][:, B], func=ACT.Identity, bias=nmr[:], scale=rstd[m][:])
            nc.gpsimd.tensor_tensor(out=ot[m][:, B], in0=ot[m][:, B], in1=gb_sb[:, 0:CW], op=ALU.mult)
            nc.gpsimd.tensor_tensor(out=ot[m][:, B], in0=ot[m][:, B], in1=gb_sb[:, CW : 2 * CW], op=ALU.add)

        def centre_scale(m, sl, g_ap):
            nc.vector.scalar_tensor_tensor(out=ot[m][:, sl], in0=yt[m][:, sl], scalar=negmean[m][:], in1=g_ap, op0=ALU.add, op1=ALU.mult)

        def norm_shift(m, sl, b_ap):
            nc.vector.scalar_tensor_tensor(out=ot[m][:, sl], in0=ot[m][:, sl], scalar=rstd[m][:], in1=b_ap, op0=ALU.mult, op1=ALU.add)

        owed = []

        def pay():
            for m, sl in owed:
                nc.sync.dma_start(out=out_1[m][:, sl], in_=o8[m][:, sl].bitcast(U8))
            owed.clear()

        def leave(m, sl):
            nc.scalar.activation(out=o8[m][:, sl], in_=ot[m][:, sl], func=ACT.Copy, scale=Y_SCALE, saturate=False)
            nc.sync.dma_start(out=out_0[m][:, sl], in_=ot[m][:, sl])
            pay()
            owed.append((m, sl))

        def turn_w1(j, g, on_vector):
            words = wraw[j][:].bitcast(F32)
            return turn([(words[:, 0, :], g), (words[:, 1, :], g)], on_vector)

        def quant_w1(j, g, grp):
            n, a = j // 2, j % 2
            nc.vector.quantize_mx(
                out=wq[n][:, g, a * 256 : (a + 1) * 256].bitcast(FP8X4),
                scales=ws[n][:, g, a * 256 : (a + 1) * 256],
                in_=grp[:].rearrange("p a r t -> p (a r t)"),
            )

        def open_acc(m, n):
            accs[(m, n)] = work.tile([P, CW], F32, name="wk", tag="wk")

        def mx_pass(m, n, g):
            nc.tensor.matmul_mx(
                out=accs[(m, n)][:],
                lhsT=cq[m][:, g, :].bitcast(FP8X4),
                lhsT_scale=cs[m][:, g, :],
                rhs=wq[n][:, g, :].bitcast(FP8X4),
                rhs_scale=ws[n][:, g, :],
                start=(g == 0),
                stop=(g == NG - 1),
            )

        def hold_gpsimd(m):
            nc.vector.tensor_copy(out=yt[m][:, 0:1], in_=eps[:])

        def bias_on_gpsimd(m, sl):
            nc.gpsimd.tensor_tensor(out=yt[m][:, sl], in0=feat[m][:, sl], in1=bo_bc[:, sl], op=ALU.add)

        nmrs = [keep.tile([P, 1], F32, name="nmr%d" % m, tag="nmr%d" % m) for m in range(NT)]
        def finish_chunk(m):
            nc.scalar.activation(out=nmrs[m][:], in_=negmean[m][:], func=ACT.Copy, scale=rstd[m][:])
            nc.scalar.activation(out=ot[m][:, B], in_=yt[m][:, B], func=ACT.Identity, bias=nmrs[m][:], scale=rstd[m][:])
            nc.gpsimd.tensor_tensor(out=ot[m][:, B], in0=ot[m][:, B], in1=gb_sb[:, 0:CW], op=ALU.mult)
            nc.gpsimd.tensor_tensor(out=ot[m][:, B], in0=ot[m][:, B], in1=gb_sb[:, CW : 2 * CW], op=ALU.add)

        def spread_for_gpsimd():
            ps = work.tile([P, 2 * CW], BF16, name="wk", tag="wk")
            spread(ps[:, 0:CW], 1, 2)
            spread(ps[:, CW : 2 * CW], 2, 2)
            nc.scalar.copy(out=gb_sb[:], in_=ps[:])

        negc = [keep.tile([P, 1], F32, name="negc%d" % m, tag="negc%d" % m) for m in range(NT)]
        q2 = [keep.tile([P, NC], F32, name="q2%d" % m, tag="q2%d" % m) for m in range(NT)]
        q2j = [keep.tile([P, NC], F32, name="q2j%d" % m, tag="q2j%d" % m) for m in range(NT)]
        d2 = [keep.tile([P, 1], F32, name="d2%d" % m, tag="d2%d" % m) for m in range(NT)]
        ee = [keep.tile([P, 1], F32, name="ee%d" % m, tag="ee%d" % m) for m in range(NT)]

        def pivot(m):
            nc.scalar.activation(out=negc[m][:], in_=s1[m][:, 0:1], func=ACT.Copy, scale=-1.0 / CW)

        def square(m, n):
            sl = slice(n * CW, (n + 1) * CW)
            sq = stage.tile([P, CW], BF16, name="sq", tag="sq", bufs=2)
            nc.scalar.activation(out=sq[:], in_=yt[m][:, sl], func=ACT.Square, bias=negc[m][:], scale=1.0, accum_out=q2[m][:, n : n + 1])

        def mean_of(m, on_vector):
            if on_vector:
                nc.vector.tensor_scalar(
                    out=s1j[m][:], in0=s1[m][:], scalar1=-1.0 / H, scalar2=None, op0=ALU.mult, op1=ALU.add, accum_out=negmean[m][:]
                )
            else:
                nc.scalar.activation(out=s1j[m][:], in_=s1[m][:], func=ACT.Copy, scale=-1.0 / H, accum_out=negmean[m][:])

        def spread_of(m):
            nc.scalar.activation(out=d2[m][:], in_=negmean[m][:], func=ACT.Square, bias=negc[m][:], scale=-1.0)
            nc.scalar.activation(out=q2j[m][:], in_=q2[m][:], func=ACT.Copy, scale=1.0 / H, accum_out=m2[m][:])
            nc.scalar.activation(out=ee[m][:], in_=d2[m][:], func=ACT.Copy, scale=-1.0, bias=LN_EPS)
            nc.scalar.activation(out=rstd[m][:], in_=m2[m][:], func=ACT.Abs_reciprocal_sqrt, bias=ee[m][:], scale=1.0)

        def stats(m, on_vector):
            if on_vector:
                nc.vector.tensor_scalar(
                    out=s1j[m][:], in0=s1[m][:], scalar1=-1.0 / H, scalar2=None, op0=ALU.mult, op1=ALU.add, accum_out=negmean[m][:]
                )
            else:
                nc.scalar.activation(out=s1j[m][:], in_=s1[m][:], func=ACT.Copy, scale=-1.0 / H, accum_out=negmean[m][:])
            sq = stage.tile([P, H], BF16, name="sq", tag="sq", bufs=2)
            nc.scalar.activation(out=sq[:], in_=yt[m][:], func=ACT.Square, bias=negmean[m][:], scale=1.0, accum_out=m2[m][:])
            nc.scalar.activation(out=rstd[m][:], in_=m2[m][:], func=ACT.Abs_reciprocal_sqrt, bias=eps[:], scale=1.0 / H)

        cgrp = {}
        for j in range(5):
            grps = turn_w(j)
            if j == 0:
                spread_bo()
            if j == 2:
                spread_g()
            quant_w(j, grps)
            if j >= 2:
                sl = slice((j - 2) * CW, (j - 1) * CW)
                nc.vector.tensor_tensor(out=yt[0][:, sl], in0=feat[0][:, sl], in1=bo_bc[:, sl], op=ALU.add)
        cgrp[0] = turn_c(0)
        grps = []
        for g in range(NG - 1):
            grps.append(turn_w1(5, g, False))
            spread(gb_ps[:, g * CW : (g + 1) * CW], 1 + g, 2)
        words5 = wraw[5][:].bitcast(F32)
        halves = [turn([(words5[:, a, :], NG - 1)], False) for a in range(2)]
        quant_c(0, cgrp[0])
        for g in range(NG - 1):
            quant_w1(5, g, grps[g])
        for a in range(2):
            nc.vector.quantize_mx(
                out=wq[2][:, NG - 1, 256 + a * P : 256 + (a + 1) * P].bitcast(FP8X4),
                scales=ws[2][:, NG - 1, 256 + a * P : 256 + (a + 1) * P],
                in_=halves[a][:, 0].rearrange("p r t -> p (r t)"),
            )
        hold_gpsimd(1)
        bias_on_gpsimd(1, A)
        bias_on_gpsimd(1, B)
        for n in range(NC):
            product(0, n)
        residual(0, 0)
        pivot(0)
        square(0, 0)
        residual(0, 1)
        square(0, 1)
        cgrp[1] = turn_c(1)
        residual(0, 2)
        spread(b_ps[:, 0:CW], 2, 0)
        spread(b_ps[:, CW:CA], 2, 1)

        mean_of(0, True)
        square(0, 2)
        spread_of(0)
        cgrp[2] = turn_c(2)
        cgrp[3] = turn_c(3)
        centre_scale(0, A, g_ps[:])
        centre_scale(0, B, gb_ps[:, 0:CW])
        spread_for_gpsimd()
        quant_c(1, cgrp[1])
        for n in range(NC):
            product(1, n)
        norm_shift(0, A, b_ps[:])
        leave(0, A)
        quant_c(2, cgrp[2])
        quant_c(3, cgrp[3])
        hold_gpsimd(2)
        for m in (2, 3):
            bias_on_gpsimd(m, A)
            bias_on_gpsimd(m, B)
        for n in range(NC):
            product(2, n)
        for n in range(NC):
            residual(1, n)
        stats(1, False)
        norm_shift(0, B, gb_ps[:, CW : 2 * CW])
        leave(0, B)
        finish_chunk(1)
        centre_scale(1, A, g_ps[:])
        for n in range(NC):
            product(3, n)
        for n in range(NC):
            residual(2, n)
        stats(2, False)
        norm_shift(1, A, b_ps[:])
        leave(1, A)
        centre_scale(2, A, g_ps[:])
        centre_scale(2, B, gb_ps[:, 0:CW])
        pay()
        for n in range(NC):
            residual(3, n)
        stats(3, False)
        leave(1, B)
        norm_shift(2, A, b_ps[:])
        leave(2, A)
        norm_shift(2, B, gb_ps[:, CW : 2 * CW])
        leave(2, B)
        centre_scale(3, A, g_ps[:])
        centre_scale(3, B, gb_ps[:, 0:CW])
        m = NT - 1
        norm_shift(m, slice(0, CW), b_ps[:, 0:CW])
        leave(m, slice(0, CW))
        norm_shift(m, slice(CW, CA), b_ps[:, CW:CA])
        nc.sync.dma_start(out=out_0[m][:, CW:CA], in_=ot[m][:, CW:CA])
        norm_shift(m, B, gb_ps[:, CW : 2 * CW])
        nc.sync.dma_start(out=out_0[m][:, B], in_=ot[m][:, B])
        pay()
        nc.vector.tensor_scalar(out=o8[m][:, CW:H], in0=ot[m][:, CW:H], scalar1=Y_SCALE, scalar2=None, op0=ALU.mult, saturate=False)
        nc.sync.dma_start(out=out_1[m][:, CW:H], in_=o8[m][:, CW:H].bitcast(U8))
